import numpy as np
import ml_dtypes


def mxq(x, axis, fmt="e4m3"):
    dtype, down = {"e4m3": (ml_dtypes.float8_e4m3fn, 7), "e5m2": (ml_dtypes.float8_e5m2, 14)}[fmt]
    v = np.moveaxis(np.asarray(x, np.float32).astype(ml_dtypes.bfloat16).astype(np.float64), axis, -1)
    blocks = v.reshape(v.shape[:-1] + (-1, 32))
    amax = np.abs(blocks).max(-1, keepdims=True)
    byte = np.maximum(np.where(amax > 0, np.frexp(amax)[1] - 1 + 127, 0) - down, 1)
    scale = np.exp2(byte - 127.0)
    codes = (blocks / scale).astype(np.float32).astype(dtype).astype(np.float64)
    return np.moveaxis((codes * scale).reshape(v.shape), -1, axis)


WIDE = False


def mx_kscale(k):
    if not WIDE:
        return np.ones(k)
    levels = np.array([10, -10, 5, -5, 0])
    a = np.random.permutation(np.resize(levels, k // 512 * 4)).reshape(k // 512, 4)
    idx = np.arange(k)
    return np.exp2(a[idx // 512, idx % 128 // 32])


BF16 = ml_dtypes.bfloat16


def bf(x):
    return np.asarray(x, np.float32).astype(BF16)


def f64(x):
    return np.asarray(x).astype(np.float64)


N, E, G, M, H = 4096, 512, 512, 256, 1
HG = H * G


def sigmoid(v):
    return 1.0 / (1.0 + np.exp(-v))


def setup_inputs():
    r = np.random.standard_normal
    s = mx_kscale(E)
    t = np.tile(mx_kscale(G), H)
    return {"q": bf(r((N, E)) * s),
            "rep": bf(r((N, E)) * s),
            "Wq": bf(r((E, HG)) * G ** 0.25 / np.sqrt(E) / s[:, None]),
            "Wk": bf(r((E, HG)) * G ** 0.25 / np.sqrt(E) / s[:, None]),
            "Wv": bf(r((E, HG)) / np.sqrt(E) / s[:, None] * t),
            "W1": bf(r((H, G, M)) * 2.0 / np.sqrt(G) / t.reshape(H, G, 1)),
            "b1": bf(r((H, M)) * 0.2)}


def reference(q, rep, Wq, Wk, Wv, W1, b1):
    qq = mxq(f64(q), 1, "e4m3")
    rq = mxq(f64(rep), 1, "e4m3")
    Qh = (qq @ mxq(f64(Wq), 0, "e4m3")).reshape(N, H, G)
    Kh = (rq @ mxq(f64(Wk), 0, "e4m3")).reshape(N, H, G)
    Vh = (rq @ mxq(f64(Wv), 0, "e4m3")).reshape(N, H, G)
    gate = sigmoid(Qh * Kh * (1.0 / np.sqrt(G)))
    z = gate * Vh
    zt = z.transpose(1, 0, 2)
    pre = (mxq(zt, 2, "e4m3") @ mxq(f64(W1), 1, "e4m3")).transpose(1, 0, 2)
    return np.maximum(pre + f64(b1), 0.0)

@@ -1,0 +1,289 @@
+import math
+from contextlib import ExitStack
+
+import concourse.mybir as mybir
+from concourse.masks import make_identity
+
+F32 = mybir.dt.float32
+BF16 = mybir.dt.bfloat16
+U32 = mybir.dt.uint32
+U8 = mybir.dt.uint8
+FP8X4 = mybir.dt.float8_e4m3fn_x4
+ALU = mybir.AluOpType
+ACT = mybir.ActivationFunctionType
+
+P = 128
+NODES, E, G, M = 4096, 512, 512, 256
+TILES = NODES // P
+PAIRS = TILES // 2
+FLOPS = 2 * NODES * E * 3 * G + 2 * NODES * G * M
+
+CHUNKS = [(0, 2), (2, 4)] + [(j, j + 4) for j in range(4, TILES, 4)]
+
+
+def tile_treehopnode_pa_t_kernel(tc, q, rep, Wq, Wk, Wv, W1, b1, out):
+    nc = tc.nc
+    q_view = q.rearrange("(p j) e -> p j e", j=TILES)
+    rep_view = rep.rearrange("(p j) e -> p j e", j=TILES)
+    out_view = out.rearrange("(p j) h m -> p j (h m)", j=TILES)
+
+    with ExitStack() as ctx:
+        const = ctx.enter_context(tc.tile_pool(name="const", bufs=1))
+        grp_pool = ctx.enter_context(tc.tile_pool(name="grp_pool", bufs=3))
+        code_pool = ctx.enter_context(tc.tile_pool(name="code_pool", bufs=4))
+        f32_pool = ctx.enter_context(tc.tile_pool(name="f32_pool", bufs=3))
+        z_pool = ctx.enter_context(tc.tile_pool(name="z_pool", bufs=3))
+        o_pool = ctx.enter_context(tc.tile_pool(name="o_pool", bufs=4))
+        tb_pool = ctx.enter_context(tc.psum_pool(name="tb_pool", bufs=2))
+        qb_pool = ctx.enter_context(tc.psum_pool(name="qb_pool", bufs=2))
+        kb_pool = ctx.enter_context(tc.psum_pool(name="kb_pool", bufs=2))
+        vb_pool = ctx.enter_context(tc.psum_pool(name="vb_pool", bufs=1))
+        ob_pool = ctx.enter_context(tc.psum_pool(name="ob_pool", bufs=1))
+        ctx.enter_context(tc.manual_schedule())
+
+        bias = const.tile([P, M], BF16, name="bias")
+        nc.scalar.dma_start(out=bias[:], in_=b1.rearrange("h m -> (h m)").partition_broadcast(P))
+
+        w_raw = {}
+        for key, w in (("q", Wq), ("k", Wk), ("v", Wv)):
+            w_raw[key] = const.tile([P, 4 * G], BF16, name="w_raw_" + key)
+            nc.sync.dma_start(
+                out=w_raw[key][:].rearrange("p (u x) -> p u x", u=2),
+                in_=w.rearrange("(u p e) g -> p u (e g)", u=2, e=2),
+            )
+        w1_raw = const.tile([P, 4 * M], BF16, name="w1_raw")
+        x_raw = {}
+        where = {}
+        for c, (j0, j1) in enumerate(CHUNKS):
+            for a, view in enumerate((q_view, rep_view)):
+                x_raw[(a, c)] = const.tile([P, (j1 - j0) * E], BF16, name="x_raw_%d_%d" % (a, c))
+                nc.sync.dma_start(
+                    out=x_raw[(a, c)][:].rearrange("p (j e) -> p j e", e=E),
+                    in_=view[:, j0:j1, :],
+                )
+            for j in range(j0, j1):
+                where[j] = (c, j - j0)
+            if c == 0:
+                nc.sync.dma_start(out=w1_raw[:], in_=W1.rearrange("h (p j) m -> (h p) (j m)", j=4))
+
+        ident = const.tile([P, P], F32, name="ident")
+        make_identity(nc, ident[:])
+        warm_in = const.tile([P, 1], F32, name="warm_in")
+        warm_out = const.tile([P, 1], F32, name="warm_out")
+        nc.vector.memset(warm_in[:], 0.0)
+        nc.scalar.activation(out=warm_out[:], in_=warm_in[:], func=ACT.Sigmoid)
+
+        w_grp = {}
+        w_code = {}
+        w_scale = {}
+        for key in ("q", "k", "v"):
+            w_grp[key] = const.tile([P, 4 * G], BF16, name="w_grp_" + key, align_bytes=64)
+            w_code[key] = const.tile([P, G], U32, name="w_code_" + key, align_bytes=64)
+            w_scale[key] = const.tile([P, G], U8, name="w_scale_" + key, align_bytes=64)
+        w1_grp = const.tile([P, 4 * M], BF16, name="w1_grp", align_bytes=64)
+        w1_code = const.tile([P, M], U32, name="w1_code", align_bytes=64)
+        w1_scale = const.tile([P, M], U8, name="w1_scale", align_bytes=64)
+
+        def regroup_w(key):
+            src = w_raw[key][:].rearrange("p (j c t) -> p t c j", j=4, t=4)
+            dst = w_grp[key][:].rearrange("p (t c j) -> p t c j", t=4, j=4)
+            nc.vector.tensor_copy(out=dst[:, 0:2], in_=src[:, 0:2])
+            nc.scalar.copy(out=dst[:, 2:4], in_=src[:, 2:4])
+
+        def quantise_w(key):
+            nc.vector.quantize_mx(
+                out=w_code[key][:].bitcast(FP8X4), scales=w_scale[key][:], in_=w_grp[key][:]
+            )
+
+        regroup_w("q")
+        regroup_w("k")
+        quantise_w("q")
+        regroup_w("v")
+        quantise_w("k")
+        quantise_w("v")
+
+        tb = {}
+        grp = {}
+        x_code = {}
+        x_scale = {}
+        banks = {}
+        q_sb = {}
+        prod = {}
+        gate = {}
+        z_grp = {}
+        z_code = {}
+        z_scale = {}
+        o_bank = {}
+        o_sb = {}
+
+        def transposes(r):
+            for j in (2 * r, 2 * r + 1):
+                c, jj = where[j]
+                tb[j] = tb_pool.tile([P, 512], F32, name="tb")
+                for a in range(2):
+                    words = x_raw[(a, c)][:].bitcast(F32)
+                    for u in range(2):
+                        s = 2 * a + u
+                        w0 = jj * (E // 2) + u * P
+                        nc.tensor.transpose(
+                            out=tb[j][:, s * P : (s + 1) * P],
+                            in_=words[:, w0 : w0 + P],
+                            identity=ident[:],
+                        )
+
+        def evacuate(j):
+            r, i = divmod(j, 2)
+            if i == 0:
+                grp[r] = grp_pool.tile([P, 2048], BF16, name="grp", align_bytes=64)
+            nc.scalar.copy(
+                out=grp[r][:, i * 1024 : (i + 1) * 1024]
+                .bitcast(F32)
+                .rearrange("p (a n u) -> p a n u", a=2, u=2),
+                in_=tb[j][:].rearrange("p (a u n) -> p a n u", a=2, u=2),
+            )
+
+        def quantise_x(r):
+            x_code[r] = code_pool.tile([P, 512], U32, name="x_code", align_bytes=64)
+            x_scale[r] = code_pool.tile([P, 512], U8, name="x_scale", align_bytes=64)
+            nc.vector.quantize_mx(
+                out=x_code[r][:].bitcast(FP8X4), scales=x_scale[r][:], in_=grp[r][:]
+            )
+
+        def project(key, j):
+            r, i = divmod(j, 2)
+            a = 0 if key == "q" else 1
+            pool = {"q": qb_pool, "k": kb_pool, "v": vb_pool}[key]
+            bank = pool.tile([P, 512], F32, name="bank_" + key)
+            banks[(key, j)] = bank
+            c0 = (2 * i + a) * P
+            for t in range(4):
+                nc.tensor.matmul_mx(
+                    out=bank[:, t * P : (t + 1) * P],
+                    lhsT=w_code[key][:, t * P : (t + 1) * P].bitcast(FP8X4),
+                    lhsT_scale=w_scale[key][:, t * P : (t + 1) * P],
+                    rhs=x_code[r][:, c0 : c0 + P].bitcast(FP8X4),
+                    rhs_scale=x_scale[r][:, c0 : c0 + P],
+                    start=True,
+                    stop=True,
+                )
+
+        def by_node(ap):
+            return ap.rearrange("p (t n) -> p n t", t=4)
+
+        def flat(ap):
+            return ap.rearrange("p (n t) -> p n t", t=4)
+
+        def copy_q(j):
+            q_sb[j] = f32_pool.tile([P, 512], F32, name="q_sb")
+            nc.scalar.copy(out=flat(q_sb[j][:]), in_=by_node(banks[("q", j)][:]))
+
+        def product(j):
+            prod[j] = f32_pool.tile([P, 512], F32, name="prod")
+            nc.vector.tensor_tensor(
+                out=flat(prod[j][:]), in0=flat(q_sb[j][:]), in1=by_node(banks[("k", j)][:]), op=ALU.mult
+            )
+
+        def sigmoid(j):
+            gate[j] = f32_pool.tile([P, 512], F32, name="gate")
+            nc.scalar.activation(
+                out=gate[j][:], in_=prod[j][:], func=ACT.Sigmoid, scale=1.0 / math.sqrt(G)
+            )
+
+        def gated(j):
+            r, i = divmod(j, 2)
+            if i == 0:
+                z_grp[r] = z_pool.tile([P, 1024], BF16, name="z_grp", align_bytes=64)
+            nc.vector.tensor_tensor(
+                out=flat(z_grp[r][:, i * 512 : (i + 1) * 512]),
+                in0=flat(gate[j][:]),
+                in1=by_node(banks[("v", j)][:]),
+                op=ALU.mult,
+            )
+
+        def quantise_z(r):
+            z_code[r] = z_pool.tile([P, 256], U32, name="z_code", align_bytes=64)
+            z_scale[r] = z_pool.tile([P, 256], U8, name="z_scale", align_bytes=64)
+            nc.vector.quantize_mx(
+                out=z_code[r][:].bitcast(FP8X4), scales=z_scale[r][:], in_=z_grp[r][:]
+            )
+
+        def layer(r):
+            o_bank[r] = ob_pool.tile([P, 512], F32, name="o_bank")
+            for i in range(2):
+                nc.tensor.matmul_mx(
+                    out=o_bank[r][:, i * M : (i + 1) * M],
+                    lhsT=z_code[r][:, i * P : (i + 1) * P].bitcast(FP8X4),
+                    lhsT_scale=z_scale[r][:, i * P : (i + 1) * P],
+                    rhs=w1_code[:].bitcast(FP8X4),
+                    rhs_scale=w1_scale[:],
+                    start=True,
+                    stop=True,
+                )
+
+        def finish(r):
+            o_sb[r] = o_pool.tile([P, 512], F32, name="o_sb")
+            nc.vector.tensor_tensor(
+                out=o_sb[r][:].rearrange("p (i m) -> p i m", i=2),
+                in0=o_bank[r][:].rearrange("p (i m) -> p i m", i=2),
+                in1=bias[:].unsqueeze(1).to_broadcast([P, 2, M]),
+                op=ALU.add,
+            )
+            nc.gpsimd.tensor_scalar(
+                out=o_sb[r][:], in0=o_sb[r][:], scalar1=0.0, scalar2=0.0, op0=ALU.max, op1=ALU.add
+            )
+            nc.sync.dma_start(
+                out=out_view[:, 2 * r : 2 * r + 2, :],
+                in_=o_sb[r][:].rearrange("p (j m) -> p j m", m=M),
+            )
+
+        def ok(r):
+            return 0 <= r < PAIRS
+
+        for r in range(-3, PAIRS + 2):
+            if ok(r - 2):
+                layer(r - 2)
+            if ok(r):
+                copy_q(2 * r + 1)
+                product(2 * r)
+                sigmoid(2 * r)
+            if ok(r - 1):
+                gated(2 * r - 1)
+            if ok(r):
+                project("k", 2 * r + 1)
+            if ok(r + 1):
+                project("q", 2 * r + 2)
+            if ok(r - 2):
+                finish(r - 2)
+            if ok(r):
+                project("v", 2 * r)
+            if ok(r + 2):
+                evacuate(2 * r + 4)
+                evacuate(2 * r + 5)
+            if ok(r + 1):
+                project("q", 2 * r + 3)
+            if ok(r):
+                product(2 * r + 1)
+                sigmoid(2 * r + 1)
+            if ok(r + 1):
+                project("k", 2 * r + 2)
+            if ok(r):
+                gated(2 * r)
+            if ok(r + 3):
+                transposes(r + 3)
+            if ok(r):
+                project("v", 2 * r + 1)
+            if ok(r + 1):
+                copy_q(2 * r + 2)
+            if ok(r - 1):
+                quantise_z(r - 1)
+            if ok(r + 2):
+                quantise_x(r + 2)
+            if r == -2:
+                nc.vector.tensor_copy(
+                    out=w1_grp[:].rearrange("p (m j) -> p m j", j=4),
+                    in_=w1_raw[:].rearrange("p (j m) -> p m j", j=4),
+                )
+            if r == -1:
+                nc.vector.quantize_mx(
+                    out=w1_code[:].bitcast(FP8X4), scales=w1_scale[:], in_=w1_grp[:]
+                )

@@ -168,10 +168,10 @@ def tile_treehopnode_pa_t_kernel(tc, q, rep, Wq, Wk, Wv, W1, b1, out):
                 )
 
         def by_node(ap):
-            return ap.rearrange("p (t n) -> p n t", t=4)
+            return ap
 
         def flat(ap):
-            return ap.rearrange("p (n t) -> p n t", t=4)
+            return ap
 
         def copy_q(j):
             q_sb[j] = f32_pool.tile([P, 512], F32, name="q_sb")
@@ -194,9 +194,9 @@ def tile_treehopnode_pa_t_kernel(tc, q, rep, Wq, Wk, Wv, W1, b1, out):
             if i == 0:
                 z_grp[r] = z_pool.tile([P, 1024], BF16, name="z_grp", align_bytes=64)
             nc.vector.tensor_tensor(
-                out=flat(z_grp[r][:, i * 512 : (i + 1) * 512]),
-                in0=flat(gate[j][:]),
-                in1=by_node(banks[("v", j)][:]),
+                out=z_grp[r][:, i * 512 : (i + 1) * 512].rearrange("p (c i t) -> p c t i", i=4, t=4),
+                in0=gate[j][:].rearrange("p (t c i) -> p c t i", t=4, i=4),
+                in1=banks[("v", j)][:].rearrange("p (t c i) -> p c t i", t=4, i=4),
                 op=ALU.mult,
             )
 

@@ -228,9 +228,9 @@ def tile_treehopnode_pa_t_kernel(tc, q, rep, Wq, Wk, Wv, W1, b1, out):
                 in1=bias[:].unsqueeze(1).to_broadcast([P, 2, M]),
                 op=ALU.add,
             )
-            nc.gpsimd.tensor_scalar(
-                out=o_sb[r][:], in0=o_sb[r][:], scalar1=0.0, scalar2=0.0, op0=ALU.max, op1=ALU.add
-            )
+
+        def relu_store(r):
+            nc.scalar.activation(out=o_sb[r][:], in_=o_sb[r][:], func=ACT.Relu)
             nc.sync.dma_start(
                 out=out_view[:, 2 * r : 2 * r + 2, :],
                 in_=o_sb[r][:].rearrange("p (j m) -> p j m", m=M),
@@ -274,6 +274,8 @@ def tile_treehopnode_pa_t_kernel(tc, q, rep, Wq, Wk, Wv, W1, b1, out):
                 project("v", 2 * r + 1)
             if ok(r + 1):
                 copy_q(2 * r + 2)
+            if ok(r - 2):
+                relu_store(r - 2)
             if ok(r - 1):
                 quantise_z(r - 1)
             if ok(r + 2):

@@ -17,8 +17,396 @@ NODES, E, G, M = 4096, 512, 512, 256
 TILES = NODES // P
 PAIRS = TILES // 2
 FLOPS = 2 * NODES * E * 3 * G + 2 * NODES * G * M
+VQ = 3
 
 CHUNKS = [(0, 2), (2, 4)] + [(j, j + 4) for j in range(4, TILES, 4)]
+
+ORDER = [
+    ("regroup_ws", ("q",)),
+    ("transposes", (0,)),
+    ("transposes", (1,)),
+    ("evacuate", (0,)),
+    ("regroup_ws", ("k",)),
+    ("regroup_wv", ("q",)),
+    ("quantise_w", ("q",)),
+    ("regroup_wv", ("k",)),
+    ("regroup_wv", ("v",)),
+    ("evacuate", (1,)),
+    ("regroup_ws", ("v",)),
+    ("quantise_w", ("v",)),
+    ("transposes", (3,)),
+    ("transposes", (2,)),
+    ("quantise_w", ("k",)),
+    ("evacuate", (3,)),
+    ("quantise_x", (0, 0)),
+    ("project", ("q", 0)),
+    ("evacuate", (2, "V")),
+    ("quantise_x", (0, 1)),
+    ("copy_q", (0,)),
+    ("project", ("k", 0)),
+    ("project", ("q", 1)),
+    ("transposes", (4,)),
+    ("transposes", (5,)),
+    ("quantise_x", (1,)),
+    ("project", ("k", 1)),
+    ("w1_regroup", ()),
+    ("project", ("v", 0)),
+    ("product", (0,)),
+    ("copy_q", (1,)),
+    ("w1_quantise", ()),
+    ("evacuate", (4, "V")),
+    ("project", ("q", 2)),
+    ("sigmoid", (0,)),
+    ("product", (1,)),
+    ("evacuate", (5,)),
+    ("transposes", (6,)),
+    ("copy_q", (2,)),
+    ("gated", (0,)),
+    ("sigmoid", (1,)),
+    ("project", ("k", 2)),
+    ("project", ("q", 3)),
+    ("quantise_x", (2,)),
+    ("project", ("v", 1)),
+    ("copy_q", (3,)),
+    ("product", (2,)),
+    ("evacuate", (6,)),
+    ("project", ("k", 3)),
+    ("transposes", (7,)),
+    ("sigmoid", (2,)),
+    ("gated", (1,)),
+    ("quantise_z", (0,)),
+    ("evacuate", (7,)),
+    ("product", (3,)),
+    ("project", ("q", 5)),
+    ("project", ("v", 2)),
+    ("project", ("q", 4)),
+    ("gated", (2,)),
+    ("project", ("k", 4)),
+    ("quantise_x", (3,)),
+    ("transposes", (8,)),
+    ("copy_q", (4,)),
+    ("product", (4,)),
+    ("sigmoid", (3,)),
+    ("transposes", (9,)),
+    ("copy_q", (5,)),
+    ("sigmoid", (4,)),
+    ("project", ("v", 3)),
+    ("project", ("k", 5)),
+    ("evacuate", (8,)),
+    ("layer", (0,)),
+    ("gated", (3,)),
+    ("product", (5,)),
+    ("bias_add", (0,)),
+    ("project", ("q", 6)),
+    ("quantise_z", (1,)),
+    ("project", ("v", 4)),
+    ("relu_store", (0, "G")),
+    ("evacuate", (9,)),
+    ("gated", (4,)),
+    ("copy_q", (6,)),
+    ("transposes", (10,)),
+    ("project", ("k", 6)),
+    ("quantise_x", (4,)),
+    ("project", ("q", 7)),
+    ("sigmoid", (5,)),
+    ("product", (6,)),
+    ("copy_q", (7,)),
+    ("project", ("v", 5)),
+    ("layer", (1,)),
+    ("project", ("k", 7)),
+    ("gated", (5,)),
+    ("transposes", (11,)),
+    ("sigmoid", (6,)),
+    ("project", ("q", 8)),
+    ("bias_add", (1,)),
+    ("project", ("v", 6)),
+    ("evacuate", (10,)),
+    ("evacuate", (11,)),
+    ("project", ("q", 9)),
+    ("product", (7,)),
+    ("sigmoid", (7,)),
+    ("project", ("k", 8)),
+    ("gated", (6,)),
+    ("transposes", (12,)),
+    ("transposes", (13,)),
+    ("project", ("v", 7)),
+    ("copy_q", (8,)),
+    ("relu_store", (1, "G")),
+    ("quantise_z", (2,)),
+    ("quantise_x", (5,)),
+    ("layer", (2,)),
+    ("copy_q", (9,)),
+    ("product", (8,)),
+    ("sigmoid", (8,)),
+    ("gated", (7,)),
+    ("project", ("k", 9)),
+    ("project", ("q", 10)),
+    ("bias_add", (2,)),
+    ("project", ("v", 8)),
+    ("evacuate", (12,)),
+    ("evacuate", (13,)),
+    ("project", ("q", 11)),
+    ("product", (9,)),
+    ("sigmoid", (9,)),
+    ("project", ("k", 10)),
+    ("gated", (8,)),
+    ("transposes", (14,)),
+    ("transposes", (15,)),
+    ("project", ("v", 9)),
+    ("copy_q", (10,)),
+    ("relu_store", (2, "G")),
+    ("quantise_z", (3,)),
+    ("quantise_x", (6,)),
+    ("layer", (3,)),
+    ("copy_q", (11,)),
+    ("product", (10,)),
+    ("sigmoid", (10,)),
+    ("gated", (9,)),
+    ("project", ("k", 11)),
+    ("project", ("q", 12)),
+    ("bias_add", (3,)),
+    ("project", ("v", 10)),
+    ("evacuate", (14,)),
+    ("evacuate", (15,)),
+    ("project", ("q", 13)),
+    ("product", (11,)),
+    ("sigmoid", (11,)),
+    ("project", ("k", 12)),
+    ("gated", (10,)),
+    ("transposes", (16,)),
+    ("transposes", (17,)),
+    ("project", ("v", 11)),
+    ("copy_q", (12,)),
+    ("relu_store", (3, "G")),
+    ("quantise_z", (4,)),
+    ("quantise_x", (7,)),
+    ("layer", (4,)),
+    ("copy_q", (13,)),
+    ("product", (12,)),
+    ("sigmoid", (12,)),
+    ("gated", (11,)),
+    ("project", ("k", 13)),
+    ("project", ("q", 14)),
+    ("bias_add", (4,)),
+    ("project", ("v", 12)),
+    ("evacuate", (16,)),
+    ("evacuate", (17,)),
+    ("project", ("q", 15)),
+    ("product", (13,)),
+    ("sigmoid", (13,)),
+    ("project", ("k", 14)),
+    ("gated", (12,)),
+    ("transposes", (18,)),
+    ("transposes", (19,)),
+    ("project", ("v", 13)),
+    ("copy_q", (14,)),
+    ("relu_store", (4, "G")),
+    ("quantise_z", (5,)),
+    ("quantise_x", (8,)),
+    ("layer", (5,)),
+    ("copy_q", (15,)),
+    ("product", (14,)),
+    ("sigmoid", (14,)),
+    ("gated", (13,)),
+    ("project", ("k", 15)),
+    ("project", ("q", 16)),
+    ("bias_add", (5,)),
+    ("project", ("v", 14)),
+    ("evacuate", (18,)),
+    ("evacuate", (19,)),
+    ("project", ("q", 17)),
+    ("product", (15,)),
+    ("sigmoid", (15,)),
+    ("project", ("k", 16)),
+    ("gated", (14,)),
+    ("transposes", (20,)),
+    ("transposes", (21,)),
+    ("project", ("v", 15)),
+    ("copy_q", (16,)),
+    ("relu_store", (5, "G")),
+    ("quantise_z", (6,)),
+    ("quantise_x", (9,)),
+    ("layer", (6,)),
+    ("copy_q", (17,)),
+    ("product", (16,)),
+    ("sigmoid", (16,)),
+    ("gated", (15,)),
+    ("project", ("k", 17)),
+    ("project", ("q", 18)),
+    ("bias_add", (6,)),
+    ("project", ("v", 16)),
+    ("evacuate", (20,)),
+    ("evacuate", (21,)),
+    ("project", ("q", 19)),
+    ("product", (17,)),
+    ("sigmoid", (17,)),
+    ("project", ("k", 18)),
+    ("gated", (16,)),
+    ("transposes", (22,)),
+    ("transposes", (23,)),
+    ("project", ("v", 17)),
+    ("copy_q", (18,)),
+    ("relu_store", (6, "G")),
+    ("quantise_z", (7,)),
+    ("quantise_x", (10,)),
+    ("layer", (7,)),
+    ("copy_q", (19,)),
+    ("product", (18,)),
+    ("sigmoid", (18,)),
+    ("gated", (17,)),
+    ("project", ("k", 19)),
+    ("project", ("q", 20)),
+    ("bias_add", (7,)),
+    ("project", ("v", 18)),
+    ("evacuate", (22,)),
+    ("evacuate", (23,)),
+    ("project", ("q", 21)),
+    ("product", (19,)),
+    ("sigmoid", (19,)),
+    ("project", ("k", 20)),
+    ("gated", (18,)),
+    ("transposes", (24,)),
+    ("transposes", (25,)),
+    ("project", ("v", 19)),
+    ("copy_q", (20,)),
+    ("relu_store", (7, "G")),
+    ("quantise_z", (8,)),
+    ("quantise_x", (11,)),
+    ("layer", (8,)),
+    ("copy_q", (21,)),
+    ("product", (20,)),
+    ("sigmoid", (20,)),
+    ("gated", (19,)),
+    ("project", ("k", 21)),
+    ("project", ("q", 22)),
+    ("bias_add", (8,)),
+    ("project", ("v", 20)),
+    ("evacuate", (24,)),
+    ("evacuate", (25,)),
+    ("project", ("q", 23)),
+    ("product", (21,)),
+    ("sigmoid", (21,)),
+    ("project", ("k", 22)),
+    ("gated", (20,)),
+    ("transposes", (26,)),
+    ("transposes", (27,)),
+    ("project", ("v", 21)),
+    ("copy_q", (22,)),
+    ("relu_store", (8, "G")),
+    ("quantise_z", (9,)),
+    ("quantise_x", (12,)),
+    ("layer", (9,)),
+    ("copy_q", (23,)),
+    ("product", (22,)),
+    ("sigmoid", (22,)),
+    ("gated", (21,)),
+    ("project", ("k", 23)),
+    ("project", ("q", 24)),
+    ("bias_add", (9,)),
+    ("project", ("v", 22)),
+    ("evacuate", (26,)),
+    ("evacuate", (27,)),
+    ("project", ("q", 25)),
+    ("product", (23,)),
+    ("sigmoid", (23,)),
+    ("project", ("k", 24)),
+    ("gated", (22,)),
+    ("transposes", (28,)),
+    ("transposes", (29,)),
+    ("project", ("v", 23)),
+    ("copy_q", (24,)),
+    ("relu_store", (9, "G")),
+    ("quantise_z", (10,)),
+    ("quantise_x", (13,)),
+    ("layer", (10,)),
+    ("copy_q", (25,)),
+    ("product", (24,)),
+    ("sigmoid", (24,)),
+    ("gated", (23,)),
+    ("project", ("k", 25)),
+    ("project", ("q", 26)),
+    ("bias_add", (10,)),
+    ("project", ("v", 24)),
+    ("evacuate", (28,)),
+    ("evacuate", (29,)),
+    ("project", ("q", 27)),
+    ("product", (25,)),
+    ("sigmoid", (25,)),
+    ("project", ("k", 26)),
+    ("gated", (24,)),
+    ("transposes", (30,)),
+    ("transposes", (31,)),
+    ("project", ("k", 27)),
+    ("copy_q", (26,)),
+    ("project", ("v", 25)),
+    ("quantise_z", (11,)),
+    ("layer", (11,)),
+    ("quantise_x", (14,)),
+    ("product", (26,)),
+    ("gated", (25,)),
+    ("project", ("q", 29)),
+    ("bias_add", (11,)),
+    ("project", ("v", 26)),
+    ("copy_q", (27,)),
+    ("quantise_z", (12,)),
+    ("sigmoid", (26,)),
+    ("product", (27,)),
+    ("project", ("k", 28)),
+    ("relu_store", (11, "G")),
+    ("project", ("q", 28)),
+    ("evacuate", (31,)),
+    ("gated", (26,)),
+    ("evacuate", (30,)),
+    ("quantise_x", (15,)),
+    ("project", ("k", 29)),
+    ("layer", (12,)),
+    ("project", ("v", 27)),
+    ("copy_q", (28,)),
+    ("sigmoid", (27,)),
+    ("product", (28,)),
+    ("relu_store", (10, "G")),
+    ("copy_q", (29,)),
+    ("gated", (27,)),
+    ("product", (29,)),
+    ("bias_add", (12,)),
+    ("sigmoid", (28,)),
+    ("project", ("q", 30)),
+    ("copy_q", (30,)),
+    ("project", ("k", 30)),
+    ("project", ("v", 28)),
+    ("project", ("k", 31)),
+    ("project", ("q", 31)),
+    ("gated", (28,)),
+    ("quantise_z", (13,)),
+    ("product", (30,)),
+    ("project", ("v", 29)),
+    ("sigmoid", (29,)),
+    ("copy_q", (31,)),
+    ("gated", (29,)),
+    ("sigmoid", (30,)),
+    ("layer", (13,)),
+    ("bias_add", (13,)),
+    ("quantise_z", (14,)),
+    ("project", ("v", 30)),
+    ("product", (31,)),
+    ("relu_store", (13, "S")),
+    ("relu_store", (12, "G")),
+    ("gated", (30,)),
+    ("sigmoid", (31,)),
+    ("layer", (14,)),
+    ("bias_add", (14,)),
+    ("project", ("v", 31)),
+    ("quantise_z", (15, 0)),
+    ("gated", (31,)),
+    ("layer", (15, 0)),
+    ("quantise_z", (15, 1)),
+    ("relu_store", (14, "S")),
+    ("bias_add", (15, 0)),
+    ("relu_store", (15, "V", 0)),
+    ("layer", (15, 1)),
+    ("bias_add", (15, 1)),
+    ("relu_store", (15, "S", 1)),
+]
 
 
 def tile_treehopnode_pa_t_kernel(tc, q, rep, Wq, Wk, Wv, W1, b1, out):
@@ -45,16 +433,19 @@ def tile_treehopnode_pa_t_kernel(tc, q, rep, Wq, Wk, Wv, W1, b1, out):
         nc.scalar.dma_start(out=bias[:], in_=b1.rearrange("h m -> (h m)").partition_broadcast(P))
 
         w_raw = {}
-        for key, w in (("q", Wq), ("k", Wk), ("v", Wv)):
+        x_raw = {}
+        where = {}
+        w1_raw = const.tile([P, 4 * M], BF16, name="w1_raw")
+
+        def load_w(key, w):
             w_raw[key] = const.tile([P, 4 * G], BF16, name="w_raw_" + key)
             nc.sync.dma_start(
                 out=w_raw[key][:].rearrange("p (u x) -> p u x", u=2),
                 in_=w.rearrange("(u p e) g -> p u (e g)", u=2, e=2),
             )
-        w1_raw = const.tile([P, 4 * M], BF16, name="w1_raw")
-        x_raw = {}
-        where = {}
-        for c, (j0, j1) in enumerate(CHUNKS):
+
+        def load_x(c):
+            j0, j1 = CHUNKS[c]
             for a, view in enumerate((q_view, rep_view)):
                 x_raw[(a, c)] = const.tile([P, (j1 - j0) * E], BF16, name="x_raw_%d_%d" % (a, c))
                 nc.sync.dma_start(
@@ -63,8 +454,20 @@ def tile_treehopnode_pa_t_kernel(tc, q, rep, Wq, Wk, Wv, W1, b1, out):
                 )
             for j in range(j0, j1):
                 where[j] = (c, j - j0)
-            if c == 0:
-                nc.sync.dma_start(out=w1_raw[:], in_=W1.rearrange("h (p j) m -> (h p) (j m)", j=4))
+
+        load_w("q", Wq)
+        load_x(0)
+        load_w("k", Wk)
+        load_w("v", Wv)
+        load_x(1)
+        nc.sync.dma_start(out=w1_raw[:], in_=W1.rearrange("h (p j) m -> (h p) (j m)", j=4))
+        load_x(2)
+        load_x(3)
+        load_x(4)
+        load_x(5)
+        load_x(6)
+        load_x(7)
+        load_x(8)
 
         ident = const.tile([P, P], F32, name="ident")
         make_identity(nc, ident[:])
@@ -84,23 +487,32 @@ def tile_treehopnode_pa_t_kernel(tc, q, rep, Wq, Wk, Wv, W1, b1, out):
         w1_code = const.tile([P, M], U32, name="w1_code", align_bytes=64)
         w1_scale = const.tile([P, M], U8, name="w1_scale", align_bytes=64)
 
-        def regroup_w(key):
+        def w_views(key):
             src = w_raw[key][:].rearrange("p (j c t) -> p t c j", j=4, t=4)
             dst = w_grp[key][:].rearrange("p (t c j) -> p t c j", t=4, j=4)
-            nc.vector.tensor_copy(out=dst[:, 0:2], in_=src[:, 0:2])
-            nc.scalar.copy(out=dst[:, 2:4], in_=src[:, 2:4])
+            return src, dst
+
+        def regroup_wv(key):
+            src, dst = w_views(key)
+            nc.vector.tensor_copy(out=dst[:, 0:VQ], in_=src[:, 0:VQ])
+
+        def regroup_ws(key):
+            src, dst = w_views(key)
+            nc.scalar.copy(out=dst[:, VQ:4], in_=src[:, VQ:4])
 
         def quantise_w(key):
             nc.vector.quantize_mx(
                 out=w_code[key][:].bitcast(FP8X4), scales=w_scale[key][:], in_=w_grp[key][:]
             )
 
-        regroup_w("q")
-        regroup_w("k")
-        quantise_w("q")
-        regroup_w("v")
-        quantise_w("k")
-        quantise_w("v")
+        def w1_regroup():
+            nc.vector.tensor_copy(
+                out=w1_grp[:].rearrange("p (m j) -> p m j", j=4),
+                in_=w1_raw[:].rearrange("p (j m) -> p m j", j=4),
+            )
+
+        def w1_quantise():
+            nc.vector.quantize_mx(out=w1_code[:].bitcast(FP8X4), scales=w1_scale[:], in_=w1_grp[:])
 
         tb = {}
         grp = {}
@@ -116,37 +528,44 @@ def tile_treehopnode_pa_t_kernel(tc, q, rep, Wq, Wk, Wv, W1, b1, out):
         o_bank = {}
         o_sb = {}
 
-        def transposes(r):
-            for j in (2 * r, 2 * r + 1):
-                c, jj = where[j]
-                tb[j] = tb_pool.tile([P, 512], F32, name="tb")
-                for a in range(2):
-                    words = x_raw[(a, c)][:].bitcast(F32)
-                    for u in range(2):
-                        s = 2 * a + u
-                        w0 = jj * (E // 2) + u * P
-                        nc.tensor.transpose(
-                            out=tb[j][:, s * P : (s + 1) * P],
-                            in_=words[:, w0 : w0 + P],
-                            identity=ident[:],
-                        )
+        def transposes(j):
+            c, jj = where[j]
+            tb[j] = tb_pool.tile([P, 512], F32, name="tb")
+            for a in range(2):
+                words = x_raw[(a, c)][:].bitcast(F32)
+                for u in range(2):
+                    s = 2 * a + u
+                    w0 = jj * (E // 2) + u * P
+                    nc.tensor.transpose(
+                        out=tb[j][:, s * P : (s + 1) * P],
+                        in_=words[:, w0 : w0 + P],
+                        identity=ident[:],
+                    )
 
-        def evacuate(j):
+        def evacuate(j, eng="S"):
             r, i = divmod(j, 2)
-            if i == 0:
+            if r not in grp:
                 grp[r] = grp_pool.tile([P, 2048], BF16, name="grp", align_bytes=64)
-            nc.scalar.copy(
-                out=grp[r][:, i * 1024 : (i + 1) * 1024]
+            dst = (
+                grp[r][:, i * 1024 : (i + 1) * 1024]
                 .bitcast(F32)
-                .rearrange("p (a n u) -> p a n u", a=2, u=2),
-                in_=tb[j][:].rearrange("p (a u n) -> p a n u", a=2, u=2),
+                .rearrange("p (a n u) -> p a n u", a=2, u=2)
             )
+            src = tb[j][:].rearrange("p (a u n) -> p a n u", a=2, u=2)
+            if eng == "S":
+                nc.scalar.copy(out=dst, in_=src)
+            else:
+                nc.vector.tensor_copy(out=dst, in_=src)
 
-        def quantise_x(r):
-            x_code[r] = code_pool.tile([P, 512], U32, name="x_code", align_bytes=64)
-            x_scale[r] = code_pool.tile([P, 512], U8, name="x_scale", align_bytes=64)
+        def quantise_x(r, half=None):
+            if r not in x_code:
+                x_code[r] = code_pool.tile([P, 512], U32, name="x_code", align_bytes=64)
+                x_scale[r] = code_pool.tile([P, 512], U8, name="x_scale", align_bytes=64)
+            lo, hi = (0, 512) if half is None else (half * 256, half * 256 + 256)
             nc.vector.quantize_mx(
-                out=x_code[r][:].bitcast(FP8X4), scales=x_scale[r][:], in_=grp[r][:]
+                out=x_code[r][:, lo:hi].bitcast(FP8X4),
+                scales=x_scale[r][:, lo:hi],
+                in_=grp[r][:, 4 * lo : 4 * hi],
             )
 
         def project(key, j):
@@ -167,20 +586,14 @@ def tile_treehopnode_pa_t_kernel(tc, q, rep, Wq, Wk, Wv, W1, b1, out):
                     stop=True,
                 )
 
-        def by_node(ap):
-            return ap
-
-        def flat(ap):
-            return ap
-
         def copy_q(j):
             q_sb[j] = f32_pool.tile([P, 512], F32, name="q_sb")
-            nc.scalar.copy(out=flat(q_sb[j][:]), in_=by_node(banks[("q", j)][:]))
+            nc.scalar.copy(out=q_sb[j][:], in_=banks[("q", j)][:])
 
         def product(j):
             prod[j] = f32_pool.tile([P, 512], F32, name="prod")
             nc.vector.tensor_tensor(
-                out=flat(prod[j][:]), in0=flat(q_sb[j][:]), in1=by_node(banks[("k", j)][:]), op=ALU.mult
+                out=prod[j][:], in0=q_sb[j][:], in1=banks[("k", j)][:], op=ALU.mult
             )
 
         def sigmoid(j):
@@ -191,7 +604,7 @@ def tile_treehopnode_pa_t_kernel(tc, q, rep, Wq, Wk, Wv, W1, b1, out):
 
         def gated(j):
             r, i = divmod(j, 2)
-            if i == 0:
+            if r not in z_grp:
                 z_grp[r] = z_pool.tile([P, 1024], BF16, name="z_grp", align_bytes=64)
             nc.vector.tensor_tensor(
                 out=z_grp[r][:, i * 512 : (i + 1) * 512].rearrange("p (c i t) -> p c t i", i=4, t=4),
@@ -200,18 +613,24 @@ def tile_treehopnode_pa_t_kernel(tc, q, rep, Wq, Wk, Wv, W1, b1, out):
                 op=ALU.mult,
             )
 
-        def quantise_z(r):
-            z_code[r] = z_pool.tile([P, 256], U32, name="z_code", align_bytes=64)
-            z_scale[r] = z_pool.tile([P, 256], U8, name="z_scale", align_bytes=64)
+        def quantise_z(r, half=None):
+            if r not in z_code:
+                z_code[r] = z_pool.tile([P, 256], U32, name="z_code", align_bytes=64)
+                z_scale[r] = z_pool.tile([P, 256], U8, name="z_scale", align_bytes=64)
+            lo, hi = (0, 256) if half is None else (half * P, half * P + P)
             nc.vector.quantize_mx(
-                out=z_code[r][:].bitcast(FP8X4), scales=z_scale[r][:], in_=z_grp[r][:]
+                out=z_code[r][:, lo:hi].bitcast(FP8X4),
+                scales=z_scale[r][:, lo:hi],
+                in_=z_grp[r][:, 4 * lo : 4 * hi],
             )
 
-        def layer(r):
-            o_bank[r] = ob_pool.tile([P, 512], F32, name="o_bank")
-            for i in range(2):
+        def layer(r, half=None):
+            tiles = (0, 1) if half is None else (half,)
+            bank = ob_pool.tile([P, 512], F32, name="o_bank")
+            o_bank[(r, half)] = bank
+            for n, i in enumerate(tiles):
                 nc.tensor.matmul_mx(
-                    out=o_bank[r][:, i * M : (i + 1) * M],
+                    out=bank[:, n * M : (n + 1) * M],
                     lhsT=z_code[r][:, i * P : (i + 1) * P].bitcast(FP8X4),
                     lhsT_scale=z_scale[r][:, i * P : (i + 1) * P],
                     rhs=w1_code[:].bitcast(FP8X4),
@@ -220,72 +639,52 @@ def tile_treehopnode_pa_t_kernel(tc, q, rep, Wq, Wk, Wv, W1, b1, out):
                     stop=True,
                 )
 
-        def finish(r):
-            o_sb[r] = o_pool.tile([P, 512], F32, name="o_sb")
+        def bias_add(r, half=None):
+            n = 2 if half is None else 1
+            res = o_pool.tile([P, 512], F32, name="o_sb")
+            o_sb[(r, half)] = res
             nc.vector.tensor_tensor(
-                out=o_sb[r][:].rearrange("p (i m) -> p i m", i=2),
-                in0=o_bank[r][:].rearrange("p (i m) -> p i m", i=2),
-                in1=bias[:].unsqueeze(1).to_broadcast([P, 2, M]),
+                out=res[:, 0 : n * M].rearrange("p (i m) -> p i m", i=n),
+                in0=o_bank[(r, half)][:, 0 : n * M].rearrange("p (i m) -> p i m", i=n),
+                in1=bias[:].unsqueeze(1).to_broadcast([P, n, M]),
                 op=ALU.add,
             )
 
-        def relu_store(r):
-            nc.scalar.activation(out=o_sb[r][:], in_=o_sb[r][:], func=ACT.Relu)
+        def relu_store(r, eng="G", half=None):
+            n = 2 if half is None else 1
+            j0 = 2 * r if half is None else 2 * r + half
+            res = o_sb[(r, half)][:, 0 : n * M]
+            if eng == "G":
+                nc.gpsimd.tensor_scalar(
+                    out=res, in0=res, scalar1=0.0, scalar2=0.0, op0=ALU.max, op1=ALU.add
+                )
+            elif eng == "S":
+                nc.scalar.activation(out=res, in_=res, func=ACT.Relu)
+            else:
+                nc.vector.tensor_scalar_max(out=res, in0=res, scalar1=0.0)
             nc.sync.dma_start(
-                out=out_view[:, 2 * r : 2 * r + 2, :],
-                in_=o_sb[r][:].rearrange("p (j m) -> p j m", m=M),
+                out=out_view[:, j0 : j0 + n, :],
+                in_=res.rearrange("p (j m) -> p j m", m=M),
             )
 
-        def ok(r):
-            return 0 <= r < PAIRS
-
-        for r in range(-3, PAIRS + 2):
-            if ok(r - 2):
-                layer(r - 2)
-            if ok(r):
-                copy_q(2 * r + 1)
-                product(2 * r)
-                sigmoid(2 * r)
-            if ok(r - 1):
-                gated(2 * r - 1)
-            if ok(r):
-                project("k", 2 * r + 1)
-            if ok(r + 1):
-                project("q", 2 * r + 2)
-            if ok(r - 2):
-                finish(r - 2)
-            if ok(r):
-                project("v", 2 * r)
-            if ok(r + 2):
-                evacuate(2 * r + 4)
-                evacuate(2 * r + 5)
-            if ok(r + 1):
-                project("q", 2 * r + 3)
-            if ok(r):
-                product(2 * r + 1)
-                sigmoid(2 * r + 1)
-            if ok(r + 1):
-                project("k", 2 * r + 2)
-            if ok(r):
-                gated(2 * r)
-            if ok(r + 3):
-                transposes(r + 3)
-            if ok(r):
-                project("v", 2 * r + 1)
-            if ok(r + 1):
-                copy_q(2 * r + 2)
-            if ok(r - 2):
-                relu_store(r - 2)
-            if ok(r - 1):
-                quantise_z(r - 1)
-            if ok(r + 2):
-                quantise_x(r + 2)
-            if r == -2:
-                nc.vector.tensor_copy(
-                    out=w1_grp[:].rearrange("p (m j) -> p m j", j=4),
-                    in_=w1_raw[:].rearrange("p (j m) -> p m j", j=4),
-                )
-            if r == -1:
-                nc.vector.quantize_mx(
-                    out=w1_code[:].bitcast(FP8X4), scales=w1_scale[:], in_=w1_grp[:]
-                )
+        stage = {
+            "regroup_wv": regroup_wv,
+            "regroup_ws": regroup_ws,
+            "quantise_w": quantise_w,
+            "w1_regroup": w1_regroup,
+            "w1_quantise": w1_quantise,
+            "transposes": transposes,
+            "evacuate": evacuate,
+            "quantise_x": quantise_x,
+            "project": project,
+            "copy_q": copy_q,
+            "product": product,
+            "sigmoid": sigmoid,
+            "gated": gated,
+            "quantise_z": quantise_z,
+            "layer": layer,
+            "bias_add": bias_add,
+            "relu_store": relu_store,
+        }
+        for name, args in ORDER:
+            stage[name](*args)

@@ -17,396 +17,8 @@ NODES, E, G, M = 4096, 512, 512, 256
 TILES = NODES // P
 PAIRS = TILES // 2
 FLOPS = 2 * NODES * E * 3 * G + 2 * NODES * G * M
-VQ = 3
 
 CHUNKS = [(0, 2), (2, 4)] + [(j, j + 4) for j in range(4, TILES, 4)]
-
-ORDER = [
-    ("regroup_ws", ("q",)),
-    ("transposes", (0,)),
-    ("transposes", (1,)),
-    ("evacuate", (0,)),
-    ("regroup_ws", ("k",)),
-    ("regroup_wv", ("q",)),
-    ("quantise_w", ("q",)),
-    ("regroup_wv", ("k",)),
-    ("regroup_wv", ("v",)),
-    ("evacuate", (1,)),
-    ("regroup_ws", ("v",)),
-    ("quantise_w", ("v",)),
-    ("transposes", (3,)),
-    ("transposes", (2,)),
-    ("quantise_w", ("k",)),
-    ("evacuate", (3,)),
-    ("quantise_x", (0, 0)),
-    ("project", ("q", 0)),
-    ("evacuate", (2, "V")),
-    ("quantise_x", (0, 1)),
-    ("copy_q", (0,)),
-    ("project", ("k", 0)),
-    ("project", ("q", 1)),
-    ("transposes", (4,)),
-    ("transposes", (5,)),
-    ("quantise_x", (1,)),
-    ("project", ("k", 1)),
-    ("w1_regroup", ()),
-    ("project", ("v", 0)),
-    ("product", (0,)),
-    ("copy_q", (1,)),
-    ("w1_quantise", ()),
-    ("evacuate", (4, "V")),
-    ("project", ("q", 2)),
-    ("sigmoid", (0,)),
-    ("product", (1,)),
-    ("evacuate", (5,)),
-    ("transposes", (6,)),
-    ("copy_q", (2,)),
-    ("gated", (0,)),
-    ("sigmoid", (1,)),
-    ("project", ("k", 2)),
-    ("project", ("q", 3)),
-    ("quantise_x", (2,)),
-    ("project", ("v", 1)),
-    ("copy_q", (3,)),
-    ("product", (2,)),
-    ("evacuate", (6,)),
-    ("project", ("k", 3)),
-    ("transposes", (7,)),
-    ("sigmoid", (2,)),
-    ("gated", (1,)),
-    ("quantise_z", (0,)),
-    ("evacuate", (7,)),
-    ("product", (3,)),
-    ("project", ("q", 5)),
-    ("project", ("v", 2)),
-    ("project", ("q", 4)),
-    ("gated", (2,)),
-    ("project", ("k", 4)),
-    ("quantise_x", (3,)),
-    ("transposes", (8,)),
-    ("copy_q", (4,)),
-    ("product", (4,)),
-    ("sigmoid", (3,)),
-    ("transposes", (9,)),
-    ("copy_q", (5,)),
-    ("sigmoid", (4,)),
-    ("project", ("v", 3)),
-    ("project", ("k", 5)),
-    ("evacuate", (8,)),
-    ("layer", (0,)),
-    ("gated", (3,)),
-    ("product", (5,)),
-    ("bias_add", (0,)),
-    ("project", ("q", 6)),
-    ("quantise_z", (1,)),
-    ("project", ("v", 4)),
-    ("relu_store", (0, "G")),
-    ("evacuate", (9,)),
-    ("gated", (4,)),
-    ("copy_q", (6,)),
-    ("transposes", (10,)),
-    ("project", ("k", 6)),
-    ("quantise_x", (4,)),
-    ("project", ("q", 7)),
-    ("sigmoid", (5,)),
-    ("product", (6,)),
-    ("copy_q", (7,)),
-    ("project", ("v", 5)),
-    ("layer", (1,)),
-    ("project", ("k", 7)),
-    ("gated", (5,)),
-    ("transposes", (11,)),
-    ("sigmoid", (6,)),
-    ("project", ("q", 8)),
-    ("bias_add", (1,)),
-    ("project", ("v", 6)),
-    ("evacuate", (10,)),
-    ("evacuate", (11,)),
-    ("project", ("q", 9)),
-    ("product", (7,)),
-    ("sigmoid", (7,)),
-    ("project", ("k", 8)),
-    ("gated", (6,)),
-    ("transposes", (12,)),
-    ("transposes", (13,)),
-    ("project", ("v", 7)),
-    ("copy_q", (8,)),
-    ("relu_store", (1, "G")),
-    ("quantise_z", (2,)),
-    ("quantise_x", (5,)),
-    ("layer", (2,)),
-    ("copy_q", (9,)),
-    ("product", (8,)),
-    ("sigmoid", (8,)),
-    ("gated", (7,)),
-    ("project", ("k", 9)),
-    ("project", ("q", 10)),
-    ("bias_add", (2,)),
-    ("project", ("v", 8)),
-    ("evacuate", (12,)),
-    ("evacuate", (13,)),
-    ("project", ("q", 11)),
-    ("product", (9,)),
-    ("sigmoid", (9,)),
-    ("project", ("k", 10)),
-    ("gated", (8,)),
-    ("transposes", (14,)),
-    ("transposes", (15,)),
-    ("project", ("v", 9)),
-    ("copy_q", (10,)),
-    ("relu_store", (2, "G")),
-    ("quantise_z", (3,)),
-    ("quantise_x", (6,)),
-    ("layer", (3,)),
-    ("copy_q", (11,)),
-    ("product", (10,)),
-    ("sigmoid", (10,)),
-    ("gated", (9,)),
-    ("project", ("k", 11)),
-    ("project", ("q", 12)),
-    ("bias_add", (3,)),
-    ("project", ("v", 10)),
-    ("evacuate", (14,)),
-    ("evacuate", (15,)),
-    ("project", ("q", 13)),
-    ("product", (11,)),
-    ("sigmoid", (11,)),
-    ("project", ("k", 12)),
-    ("gated", (10,)),
-    ("transposes", (16,)),
-    ("transposes", (17,)),
-    ("project", ("v", 11)),
-    ("copy_q", (12,)),
-    ("relu_store", (3, "G")),
-    ("quantise_z", (4,)),
-    ("quantise_x", (7,)),
-    ("layer", (4,)),
-    ("copy_q", (13,)),
-    ("product", (12,)),
-    ("sigmoid", (12,)),
-    ("gated", (11,)),
-    ("project", ("k", 13)),
-    ("project", ("q", 14)),
-    ("bias_add", (4,)),
-    ("project", ("v", 12)),
-    ("evacuate", (16,)),
-    ("evacuate", (17,)),
-    ("project", ("q", 15)),
-    ("product", (13,)),
-    ("sigmoid", (13,)),
-    ("project", ("k", 14)),
-    ("gated", (12,)),
-    ("transposes", (18,)),
-    ("transposes", (19,)),
-    ("project", ("v", 13)),
-    ("copy_q", (14,)),
-    ("relu_store", (4, "G")),
-    ("quantise_z", (5,)),
-    ("quantise_x", (8,)),
-    ("layer", (5,)),
-    ("copy_q", (15,)),
-    ("product", (14,)),
-    ("sigmoid", (14,)),
-    ("gated", (13,)),
-    ("project", ("k", 15)),
-    ("project", ("q", 16)),
-    ("bias_add", (5,)),
-    ("project", ("v", 14)),
-    ("evacuate", (18,)),
-    ("evacuate", (19,)),
-    ("project", ("q", 17)),
-    ("product", (15,)),
-    ("sigmoid", (15,)),
-    ("project", ("k", 16)),
-    ("gated", (14,)),
-    ("transposes", (20,)),
-    ("transposes", (21,)),
-    ("project", ("v", 15)),
-    ("copy_q", (16,)),
-    ("relu_store", (5, "G")),
-    ("quantise_z", (6,)),
-    ("quantise_x", (9,)),
-    ("layer", (6,)),
-    ("copy_q", (17,)),
-    ("product", (16,)),
-    ("sigmoid", (16,)),
-    ("gated", (15,)),
-    ("project", ("k", 17)),
-    ("project", ("q", 18)),
-    ("bias_add", (6,)),
-    ("project", ("v", 16)),
-    ("evacuate", (20,)),
-    ("evacuate", (21,)),
-    ("project", ("q", 19)),
-    ("product", (17,)),
-    ("sigmoid", (17,)),
-    ("project", ("k", 18)),
-    ("gated", (16,)),
-    ("transposes", (22,)),
-    ("transposes", (23,)),
-    ("project", ("v", 17)),
-    ("copy_q", (18,)),
-    ("relu_store", (6, "G")),
-    ("quantise_z", (7,)),
-    ("quantise_x", (10,)),
-    ("layer", (7,)),
-    ("copy_q", (19,)),
-    ("product", (18,)),
-    ("sigmoid", (18,)),
-    ("gated", (17,)),
-    ("project", ("k", 19)),
-    ("project", ("q", 20)),
-    ("bias_add", (7,)),
-    ("project", ("v", 18)),
-    ("evacuate", (22,)),
-    ("evacuate", (23,)),
-    ("project", ("q", 21)),
-    ("product", (19,)),
-    ("sigmoid", (19,)),
-    ("project", ("k", 20)),
-    ("gated", (18,)),
-    ("transposes", (24,)),
-    ("transposes", (25,)),
-    ("project", ("v", 19)),
-    ("copy_q", (20,)),
-    ("relu_store", (7, "G")),
-    ("quantise_z", (8,)),
-    ("quantise_x", (11,)),
-    ("layer", (8,)),
-    ("copy_q", (21,)),
-    ("product", (20,)),
-    ("sigmoid", (20,)),
-    ("gated", (19,)),
-    ("project", ("k", 21)),
-    ("project", ("q", 22)),
-    ("bias_add", (8,)),
-    ("project", ("v", 20)),
-    ("evacuate", (24,)),
-    ("evacuate", (25,)),
-    ("project", ("q", 23)),
-    ("product", (21,)),
-    ("sigmoid", (21,)),
-    ("project", ("k", 22)),
-    ("gated", (20,)),
-    ("transposes", (26,)),
-    ("transposes", (27,)),
-    ("project", ("v", 21)),
-    ("copy_q", (22,)),
-    ("relu_store", (8, "G")),
-    ("quantise_z", (9,)),
-    ("quantise_x", (12,)),
-    ("layer", (9,)),
-    ("copy_q", (23,)),
-    ("product", (22,)),
-    ("sigmoid", (22,)),
-    ("gated", (21,)),
-    ("project", ("k", 23)),
-    ("project", ("q", 24)),
-    ("bias_add", (9,)),
-    ("project", ("v", 22)),
-    ("evacuate", (26,)),
-    ("evacuate", (27,)),
-    ("project", ("q", 25)),
-    ("product", (23,)),
-    ("sigmoid", (23,)),
-    ("project", ("k", 24)),
-    ("gated", (22,)),
-    ("transposes", (28,)),
-    ("transposes", (29,)),
-    ("project", ("v", 23)),
-    ("copy_q", (24,)),
-    ("relu_store", (9, "G")),
-    ("quantise_z", (10,)),
-    ("quantise_x", (13,)),
-    ("layer", (10,)),
-    ("copy_q", (25,)),
-    ("product", (24,)),
-    ("sigmoid", (24,)),
-    ("gated", (23,)),
-    ("project", ("k", 25)),
-    ("project", ("q", 26)),
-    ("bias_add", (10,)),
-    ("project", ("v", 24)),
-    ("evacuate", (28,)),
-    ("evacuate", (29,)),
-    ("project", ("q", 27)),
-    ("product", (25,)),
-    ("sigmoid", (25,)),
-    ("project", ("k", 26)),
-    ("gated", (24,)),
-    ("transposes", (30,)),
-    ("transposes", (31,)),
-    ("project", ("k", 27)),
-    ("copy_q", (26,)),
-    ("project", ("v", 25)),
-    ("quantise_z", (11,)),
-    ("layer", (11,)),
-    ("quantise_x", (14,)),
-    ("product", (26,)),
-    ("gated", (25,)),
-    ("project", ("q", 29)),
-    ("bias_add", (11,)),
-    ("project", ("v", 26)),
-    ("copy_q", (27,)),
-    ("quantise_z", (12,)),
-    ("sigmoid", (26,)),
-    ("product", (27,)),
-    ("project", ("k", 28)),
-    ("relu_store", (11, "G")),
-    ("project", ("q", 28)),
-    ("evacuate", (31,)),
-    ("gated", (26,)),
-    ("evacuate", (30,)),
-    ("quantise_x", (15,)),
-    ("project", ("k", 29)),
-    ("layer", (12,)),
-    ("project", ("v", 27)),
-    ("copy_q", (28,)),
-    ("sigmoid", (27,)),
-    ("product", (28,)),
-    ("relu_store", (10, "G")),
-    ("copy_q", (29,)),
-    ("gated", (27,)),
-    ("product", (29,)),
-    ("bias_add", (12,)),
-    ("sigmoid", (28,)),
-    ("project", ("q", 30)),
-    ("copy_q", (30,)),
-    ("project", ("k", 30)),
-    ("project", ("v", 28)),
-    ("project", ("k", 31)),
-    ("project", ("q", 31)),
-    ("gated", (28,)),
-    ("quantise_z", (13,)),
-    ("product", (30,)),
-    ("project", ("v", 29)),
-    ("sigmoid", (29,)),
-    ("copy_q", (31,)),
-    ("gated", (29,)),
-    ("sigmoid", (30,)),
-    ("layer", (13,)),
-    ("bias_add", (13,)),
-    ("quantise_z", (14,)),
-    ("project", ("v", 30)),
-    ("product", (31,)),
-    ("relu_store", (13, "S")),
-    ("relu_store", (12, "G")),
-    ("gated", (30,)),
-    ("sigmoid", (31,)),
-    ("layer", (14,)),
-    ("bias_add", (14,)),
-    ("project", ("v", 31)),
-    ("quantise_z", (15, 0)),
-    ("gated", (31,)),
-    ("layer", (15, 0)),
-    ("quantise_z", (15, 1)),
-    ("relu_store", (14, "S")),
-    ("bias_add", (15, 0)),
-    ("relu_store", (15, "V", 0)),
-    ("layer", (15, 1)),
-    ("bias_add", (15, 1)),
-    ("relu_store", (15, "S", 1)),
-]
 
 
 def tile_treehopnode_pa_t_kernel(tc, q, rep, Wq, Wk, Wv, W1, b1, out):
@@ -427,7 +39,6 @@ def tile_treehopnode_pa_t_kernel(tc, q, rep, Wq, Wk, Wv, W1, b1, out):
         kb_pool = ctx.enter_context(tc.psum_pool(name="kb_pool", bufs=2))
         vb_pool = ctx.enter_context(tc.psum_pool(name="vb_pool", bufs=1))
         ob_pool = ctx.enter_context(tc.psum_pool(name="ob_pool", bufs=1))
-        ctx.enter_context(tc.manual_schedule())
 
         bias = const.tile([P, M], BF16, name="bias")
         nc.scalar.dma_start(out=bias[:], in_=b1.rearrange("h m -> (h m)").partition_broadcast(P))
@@ -461,13 +72,8 @@ def tile_treehopnode_pa_t_kernel(tc, q, rep, Wq, Wk, Wv, W1, b1, out):
         load_w("v", Wv)
         load_x(1)
         nc.sync.dma_start(out=w1_raw[:], in_=W1.rearrange("h (p j) m -> (h p) (j m)", j=4))
-        load_x(2)
-        load_x(3)
-        load_x(4)
-        load_x(5)
-        load_x(6)
-        load_x(7)
-        load_x(8)
+        for c in range(2, len(CHUNKS)):
+            load_x(c)
 
         ident = const.tile([P, P], F32, name="ident")
         make_identity(nc, ident[:])
@@ -487,32 +93,23 @@ def tile_treehopnode_pa_t_kernel(tc, q, rep, Wq, Wk, Wv, W1, b1, out):
         w1_code = const.tile([P, M], U32, name="w1_code", align_bytes=64)
         w1_scale = const.tile([P, M], U8, name="w1_scale", align_bytes=64)
 
-        def w_views(key):
+        def regroup_w(key):
             src = w_raw[key][:].rearrange("p (j c t) -> p t c j", j=4, t=4)
             dst = w_grp[key][:].rearrange("p (t c j) -> p t c j", t=4, j=4)
-            return src, dst
-
-        def regroup_wv(key):
-            src, dst = w_views(key)
-            nc.vector.tensor_copy(out=dst[:, 0:VQ], in_=src[:, 0:VQ])
-
-        def regroup_ws(key):
-            src, dst = w_views(key)
-            nc.scalar.copy(out=dst[:, VQ:4], in_=src[:, VQ:4])
+            nc.vector.tensor_copy(out=dst[:, 0:3], in_=src[:, 0:3])
+            nc.scalar.copy(out=dst[:, 3:4], in_=src[:, 3:4])
 
         def quantise_w(key):
             nc.vector.quantize_mx(
                 out=w_code[key][:].bitcast(FP8X4), scales=w_scale[key][:], in_=w_grp[key][:]
             )
 
-        def w1_regroup():
-            nc.vector.tensor_copy(
-                out=w1_grp[:].rearrange("p (m j) -> p m j", j=4),
-                in_=w1_raw[:].rearrange("p (j m) -> p m j", j=4),
-            )
-
-        def w1_quantise():
-            nc.vector.quantize_mx(out=w1_code[:].bitcast(FP8X4), scales=w1_scale[:], in_=w1_grp[:])
+        regroup_w("q")
+        regroup_w("k")
+        quantise_w("q")
+        regroup_w("v")
+        quantise_w("k")
+        quantise_w("v")
 
         tb = {}
         grp = {}
@@ -528,44 +125,37 @@ def tile_treehopnode_pa_t_kernel(tc, q, rep, Wq, Wk, Wv, W1, b1, out):
         o_bank = {}
         o_sb = {}
 
-        def transposes(j):
-            c, jj = where[j]
-            tb[j] = tb_pool.tile([P, 512], F32, name="tb")
-            for a in range(2):
-                words = x_raw[(a, c)][:].bitcast(F32)
-                for u in range(2):
-                    s = 2 * a + u
-                    w0 = jj * (E // 2) + u * P
-                    nc.tensor.transpose(
-                        out=tb[j][:, s * P : (s + 1) * P],
-                        in_=words[:, w0 : w0 + P],
-                        identity=ident[:],
-                    )
+        def transposes(r):
+            for j in (2 * r, 2 * r + 1):
+                c, jj = where[j]
+                tb[j] = tb_pool.tile([P, 512], F32, name="tb")
+                for a in range(2):
+                    words = x_raw[(a, c)][:].bitcast(F32)
+                    for u in range(2):
+                        s = 2 * a + u
+                        w0 = jj * (E // 2) + u * P
+                        nc.tensor.transpose(
+                            out=tb[j][:, s * P : (s + 1) * P],
+                            in_=words[:, w0 : w0 + P],
+                            identity=ident[:],
+                        )
 
-        def evacuate(j, eng="S"):
+        def evacuate(j):
             r, i = divmod(j, 2)
-            if r not in grp:
+            if i == 0:
                 grp[r] = grp_pool.tile([P, 2048], BF16, name="grp", align_bytes=64)
-            dst = (
-                grp[r][:, i * 1024 : (i + 1) * 1024]
+            nc.scalar.copy(
+                out=grp[r][:, i * 1024 : (i + 1) * 1024]
                 .bitcast(F32)
-                .rearrange("p (a n u) -> p a n u", a=2, u=2)
+                .rearrange("p (a n u) -> p a n u", a=2, u=2),
+                in_=tb[j][:].rearrange("p (a u n) -> p a n u", a=2, u=2),
             )
-            src = tb[j][:].rearrange("p (a u n) -> p a n u", a=2, u=2)
-            if eng == "S":
-                nc.scalar.copy(out=dst, in_=src)
-            else:
-                nc.vector.tensor_copy(out=dst, in_=src)
 
-        def quantise_x(r, half=None):
-            if r not in x_code:
-                x_code[r] = code_pool.tile([P, 512], U32, name="x_code", align_bytes=64)
-                x_scale[r] = code_pool.tile([P, 512], U8, name="x_scale", align_bytes=64)
-            lo, hi = (0, 512) if half is None else (half * 256, half * 256 + 256)
+        def quantise_x(r):
+            x_code[r] = code_pool.tile([P, 512], U32, name="x_code", align_bytes=64)
+            x_scale[r] = code_pool.tile([P, 512], U8, name="x_scale", align_bytes=64)
             nc.vector.quantize_mx(
-                out=x_code[r][:, lo:hi].bitcast(FP8X4),
-                scales=x_scale[r][:, lo:hi],
-                in_=grp[r][:, 4 * lo : 4 * hi],
+                out=x_code[r][:].bitcast(FP8X4), scales=x_scale[r][:], in_=grp[r][:]
             )
 
         def project(key, j):
@@ -586,14 +176,20 @@ def tile_treehopnode_pa_t_kernel(tc, q, rep, Wq, Wk, Wv, W1, b1, out):
                     stop=True,
                 )
 
+        def by_node(ap):
+            return ap
+
+        def flat(ap):
+            return ap
+
         def copy_q(j):
             q_sb[j] = f32_pool.tile([P, 512], F32, name="q_sb")
-            nc.scalar.copy(out=q_sb[j][:], in_=banks[("q", j)][:])
+            nc.scalar.copy(out=flat(q_sb[j][:]), in_=by_node(banks[("q", j)][:]))
 
         def product(j):
             prod[j] = f32_pool.tile([P, 512], F32, name="prod")
             nc.vector.tensor_tensor(
-                out=prod[j][:], in0=q_sb[j][:], in1=banks[("k", j)][:], op=ALU.mult
+                out=flat(prod[j][:]), in0=flat(q_sb[j][:]), in1=by_node(banks[("k", j)][:]), op=ALU.mult
             )
 
         def sigmoid(j):
@@ -604,7 +200,7 @@ def tile_treehopnode_pa_t_kernel(tc, q, rep, Wq, Wk, Wv, W1, b1, out):
 
         def gated(j):
             r, i = divmod(j, 2)
-            if r not in z_grp:
+            if i == 0:
                 z_grp[r] = z_pool.tile([P, 1024], BF16, name="z_grp", align_bytes=64)
             nc.vector.tensor_tensor(
                 out=z_grp[r][:, i * 512 : (i + 1) * 512].rearrange("p (c i t) -> p c t i", i=4, t=4),
@@ -613,24 +209,18 @@ def tile_treehopnode_pa_t_kernel(tc, q, rep, Wq, Wk, Wv, W1, b1, out):
                 op=ALU.mult,
             )
 
-        def quantise_z(r, half=None):
-            if r not in z_code:
-                z_code[r] = z_pool.tile([P, 256], U32, name="z_code", align_bytes=64)
-                z_scale[r] = z_pool.tile([P, 256], U8, name="z_scale", align_bytes=64)
-            lo, hi = (0, 256) if half is None else (half * P, half * P + P)
+        def quantise_z(r):
+            z_code[r] = z_pool.tile([P, 256], U32, name="z_code", align_bytes=64)
+            z_scale[r] = z_pool.tile([P, 256], U8, name="z_scale", align_bytes=64)
             nc.vector.quantize_mx(
-                out=z_code[r][:, lo:hi].bitcast(FP8X4),
-                scales=z_scale[r][:, lo:hi],
-                in_=z_grp[r][:, 4 * lo : 4 * hi],
+                out=z_code[r][:].bitcast(FP8X4), scales=z_scale[r][:], in_=z_grp[r][:]
             )
 
-        def layer(r, half=None):
-            tiles = (0, 1) if half is None else (half,)
-            bank = ob_pool.tile([P, 512], F32, name="o_bank")
-            o_bank[(r, half)] = bank
-            for n, i in enumerate(tiles):
+        def layer(r):
+            o_bank[r] = ob_pool.tile([P, 512], F32, name="o_bank")
+            for i in range(2):
                 nc.tensor.matmul_mx(
-                    out=bank[:, n * M : (n + 1) * M],
+                    out=o_bank[r][:, i * M : (i + 1) * M],
                     lhsT=z_code[r][:, i * P : (i + 1) * P].bitcast(FP8X4),
                     lhsT_scale=z_scale[r][:, i * P : (i + 1) * P],
                     rhs=w1_code[:].bitcast(FP8X4),
@@ -639,52 +229,72 @@ def tile_treehopnode_pa_t_kernel(tc, q, rep, Wq, Wk, Wv, W1, b1, out):
                     stop=True,
                 )
 
-        def bias_add(r, half=None):
-            n = 2 if half is None else 1
-            res = o_pool.tile([P, 512], F32, name="o_sb")
-            o_sb[(r, half)] = res
+        def finish(r):
+            o_sb[r] = o_pool.tile([P, 512], F32, name="o_sb")
             nc.vector.tensor_tensor(
-                out=res[:, 0 : n * M].rearrange("p (i m) -> p i m", i=n),
-                in0=o_bank[(r, half)][:, 0 : n * M].rearrange("p (i m) -> p i m", i=n),
-                in1=bias[:].unsqueeze(1).to_broadcast([P, n, M]),
+                out=o_sb[r][:].rearrange("p (i m) -> p i m", i=2),
+                in0=o_bank[r][:].rearrange("p (i m) -> p i m", i=2),
+                in1=bias[:].unsqueeze(1).to_broadcast([P, 2, M]),
                 op=ALU.add,
             )
 
-        def relu_store(r, eng="G", half=None):
-            n = 2 if half is None else 1
-            j0 = 2 * r if half is None else 2 * r + half
-            res = o_sb[(r, half)][:, 0 : n * M]
-            if eng == "G":
-                nc.gpsimd.tensor_scalar(
-                    out=res, in0=res, scalar1=0.0, scalar2=0.0, op0=ALU.max, op1=ALU.add
-                )
-            elif eng == "S":
-                nc.scalar.activation(out=res, in_=res, func=ACT.Relu)
-            else:
-                nc.vector.tensor_scalar_max(out=res, in0=res, scalar1=0.0)
+        def relu_store(r):
+            nc.scalar.activation(out=o_sb[r][:], in_=o_sb[r][:], func=ACT.Relu)
             nc.sync.dma_start(
-                out=out_view[:, j0 : j0 + n, :],
-                in_=res.rearrange("p (j m) -> p j m", m=M),
+                out=out_view[:, 2 * r : 2 * r + 2, :],
+                in_=o_sb[r][:].rearrange("p (j m) -> p j m", m=M),
             )
 
-        stage = {
-            "regroup_wv": regroup_wv,
-            "regroup_ws": regroup_ws,
-            "quantise_w": quantise_w,
-            "w1_regroup": w1_regroup,
-            "w1_quantise": w1_quantise,
-            "transposes": transposes,
-            "evacuate": evacuate,
-            "quantise_x": quantise_x,
-            "project": project,
-            "copy_q": copy_q,
-            "product": product,
-            "sigmoid": sigmoid,
-            "gated": gated,
-            "quantise_z": quantise_z,
-            "layer": layer,
-            "bias_add": bias_add,
-            "relu_store": relu_store,
-        }
-        for name, args in ORDER:
-            stage[name](*args)
+        def ok(r):
+            return 0 <= r < PAIRS
+
+        for r in range(-3, PAIRS + 2):
+            if ok(r - 2):
+                layer(r - 2)
+            if ok(r):
+                copy_q(2 * r + 1)
+                product(2 * r)
+                sigmoid(2 * r)
+            if ok(r - 1):
+                gated(2 * r - 1)
+            if ok(r):
+                project("k", 2 * r + 1)
+            if ok(r + 1):
+                project("q", 2 * r + 2)
+            if ok(r - 2):
+                finish(r - 2)
+            if ok(r):
+                project("v", 2 * r)
+            if ok(r + 2):
+                evacuate(2 * r + 4)
+                evacuate(2 * r + 5)
+            if ok(r + 1):
+                project("q", 2 * r + 3)
+            if ok(r):
+                product(2 * r + 1)
+                sigmoid(2 * r + 1)
+            if ok(r + 1):
+                project("k", 2 * r + 2)
+            if ok(r):
+                gated(2 * r)
+            if ok(r + 3):
+                transposes(r + 3)
+            if ok(r):
+                project("v", 2 * r + 1)
+            if ok(r + 1):
+                copy_q(2 * r + 2)
+            if ok(r - 2):
+                relu_store(r - 2)
+            if ok(r - 1):
+                quantise_z(r - 1)
+            if ok(r + 2):
+                quantise_x(r + 2)
+            if r == -2:
+                nc.vector.tensor_copy(
+                    out=w1_grp[:].rearrange("p (m j) -> p m j", j=4),
+                    in_=w1_raw[:].rearrange("p (j m) -> p m j", j=4),
+                )
+            if r == -1:
+                nc.vector.quantize_mx(
+                    out=w1_code[:].bitcast(FP8X4), scales=w1_scale[:], in_=w1_grp[:]
+                )

@@ -39,24 +39,21 @@ def tile_treehopnode_pa_t_kernel(tc, q, rep, Wq, Wk, Wv, W1, b1, out):
         kb_pool = ctx.enter_context(tc.psum_pool(name="kb_pool", bufs=2))
         vb_pool = ctx.enter_context(tc.psum_pool(name="vb_pool", bufs=1))
         ob_pool = ctx.enter_context(tc.psum_pool(name="ob_pool", bufs=1))
+        ctx.enter_context(tc.manual_schedule())
 
         bias = const.tile([P, M], BF16, name="bias")
-        nc.scalar.dma_start(out=bias[:], in_=b1.rearrange("h m -> (h m)").partition_broadcast(P))
 
         w_raw = {}
-        x_raw = {}
-        where = {}
-        w1_raw = const.tile([P, 4 * M], BF16, name="w1_raw")
-
-        def load_w(key, w):
+        for key, w in (("q", Wq), ("k", Wk), ("v", Wv)):
             w_raw[key] = const.tile([P, 4 * G], BF16, name="w_raw_" + key)
             nc.sync.dma_start(
                 out=w_raw[key][:].rearrange("p (u x) -> p u x", u=2),
                 in_=w.rearrange("(u p e) g -> p u (e g)", u=2, e=2),
             )
-
-        def load_x(c):
-            j0, j1 = CHUNKS[c]
+        w1_raw = const.tile([P, 4 * M], BF16, name="w1_raw")
+        x_raw = {}
+        where = {}
+        for c, (j0, j1) in enumerate(CHUNKS):
             for a, view in enumerate((q_view, rep_view)):
                 x_raw[(a, c)] = const.tile([P, (j1 - j0) * E], BF16, name="x_raw_%d_%d" % (a, c))
                 nc.sync.dma_start(
@@ -65,15 +62,12 @@ def tile_treehopnode_pa_t_kernel(tc, q, rep, Wq, Wk, Wv, W1, b1, out):
                 )
             for j in range(j0, j1):
                 where[j] = (c, j - j0)
-
-        load_w("q", Wq)
-        load_x(0)
-        load_w("k", Wk)
-        load_w("v", Wv)
-        load_x(1)
-        nc.sync.dma_start(out=w1_raw[:], in_=W1.rearrange("h (p j) m -> (h p) (j m)", j=4))
-        for c in range(2, len(CHUNKS)):
-            load_x(c)
+            if c == 0:
+                nc.sync.dma_start(out=w1_raw[:], in_=W1.rearrange("h (p j) m -> (h p) (j m)", j=4))
+            if c == 2:
+                nc.sync.dma_start(
+                    out=bias[:], in_=b1.rearrange("h m -> (h m)").partition_broadcast(P)
+                )
 
         ident = const.tile([P, P], F32, name="ident")
         make_identity(nc, ident[:])
@@ -96,8 +90,8 @@ def tile_treehopnode_pa_t_kernel(tc, q, rep, Wq, Wk, Wv, W1, b1, out):
         def regroup_w(key):
             src = w_raw[key][:].rearrange("p (j c t) -> p t c j", j=4, t=4)
             dst = w_grp[key][:].rearrange("p (t c j) -> p t c j", t=4, j=4)
-            nc.vector.tensor_copy(out=dst[:, 0:3], in_=src[:, 0:3])
-            nc.scalar.copy(out=dst[:, 3:4], in_=src[:, 3:4])
+            nc.vector.tensor_copy(out=dst[:, 0:2], in_=src[:, 0:2])
+            nc.scalar.copy(out=dst[:, 2:4], in_=src[:, 2:4])
 
         def quantise_w(key):
             nc.vector.quantize_mx(

@@ -13,12 +13,16 @@ ALU = mybir.AluOpType
 ACT = mybir.ActivationFunctionType
 
 P = 128
+PACK = 4
+BANK = 512
 NODES, E, G, M = 4096, 512, 512, 256
 TILES = NODES // P
 PAIRS = TILES // 2
 FLOPS = 2 * NODES * E * 3 * G + 2 * NODES * G * M
 
 CHUNKS = [(0, 2), (2, 4)] + [(j, j + 4) for j in range(4, TILES, 4)]
+
+PAIRS_WITH_RELU_ON_SCALAR = 2
 
 
 def tile_treehopnode_pa_t_kernel(tc, q, rep, Wq, Wk, Wv, W1, b1, out):
@@ -42,15 +46,14 @@ def tile_treehopnode_pa_t_kernel(tc, q, rep, Wq, Wk, Wv, W1, b1, out):
         ctx.enter_context(tc.manual_schedule())
 
         bias = const.tile([P, M], BF16, name="bias")
-
         w_raw = {}
         for key, w in (("q", Wq), ("k", Wk), ("v", Wv)):
-            w_raw[key] = const.tile([P, 4 * G], BF16, name="w_raw_" + key)
+            w_raw[key] = const.tile([P, PACK * G], BF16, name="w_raw_" + key)
             nc.sync.dma_start(
                 out=w_raw[key][:].rearrange("p (u x) -> p u x", u=2),
                 in_=w.rearrange("(u p e) g -> p u (e g)", u=2, e=2),
             )
-        w1_raw = const.tile([P, 4 * M], BF16, name="w1_raw")
+        w1_raw = const.tile([P, PACK * M], BF16, name="w1_raw")
         x_raw = {}
         where = {}
         for c, (j0, j1) in enumerate(CHUNKS):
@@ -63,7 +66,7 @@ def tile_treehopnode_pa_t_kernel(tc, q, rep, Wq, Wk, Wv, W1, b1, out):
             for j in range(j0, j1):
                 where[j] = (c, j - j0)
             if c == 0:
-                nc.sync.dma_start(out=w1_raw[:], in_=W1.rearrange("h (p j) m -> (h p) (j m)", j=4))
+                nc.sync.dma_start(out=w1_raw[:], in_=W1.rearrange("h (p j) m -> (h p) (j m)", j=PACK))
             if c == 2:
                 nc.sync.dma_start(
                     out=bias[:], in_=b1.rearrange("h m -> (h m)").partition_broadcast(P)
@@ -80,16 +83,16 @@ def tile_treehopnode_pa_t_kernel(tc, q, rep, Wq, Wk, Wv, W1, b1, out):
         w_code = {}
         w_scale = {}
         for key in ("q", "k", "v"):
-            w_grp[key] = const.tile([P, 4 * G], BF16, name="w_grp_" + key, align_bytes=64)
+            w_grp[key] = const.tile([P, PACK * G], BF16, name="w_grp_" + key, align_bytes=64)
             w_code[key] = const.tile([P, G], U32, name="w_code_" + key, align_bytes=64)
             w_scale[key] = const.tile([P, G], U8, name="w_scale_" + key, align_bytes=64)
-        w1_grp = const.tile([P, 4 * M], BF16, name="w1_grp", align_bytes=64)
+        w1_grp = const.tile([P, PACK * M], BF16, name="w1_grp", align_bytes=64)
         w1_code = const.tile([P, M], U32, name="w1_code", align_bytes=64)
         w1_scale = const.tile([P, M], U8, name="w1_scale", align_bytes=64)
 
         def regroup_w(key):
-            src = w_raw[key][:].rearrange("p (j c t) -> p t c j", j=4, t=4)
-            dst = w_grp[key][:].rearrange("p (t c j) -> p t c j", t=4, j=4)
+            src = w_raw[key][:].rearrange("p (j c t) -> p t c j", j=PACK, t=4)
+            dst = w_grp[key][:].rearrange("p (t c j) -> p t c j", t=4, j=PACK)
             nc.vector.tensor_copy(out=dst[:, 0:2], in_=src[:, 0:2])
             nc.scalar.copy(out=dst[:, 2:4], in_=src[:, 2:4])
 
@@ -121,13 +124,13 @@ def tile_treehopnode_pa_t_kernel(tc, q, rep, Wq, Wk, Wv, W1, b1, out):
 
         def transposes(r):
             for j in (2 * r, 2 * r + 1):
-                c, jj = where[j]
-                tb[j] = tb_pool.tile([P, 512], F32, name="tb")
+                c, place = where[j]
+                tb[j] = tb_pool.tile([P, BANK], F32, name="tb")
                 for a in range(2):
                     words = x_raw[(a, c)][:].bitcast(F32)
                     for u in range(2):
                         s = 2 * a + u
-                        w0 = jj * (E // 2) + u * P
+                        w0 = place * (E // 2) + u * P
                         nc.tensor.transpose(
                             out=tb[j][:, s * P : (s + 1) * P],
                             in_=words[:, w0 : w0 + P],
@@ -137,17 +140,18 @@ def tile_treehopnode_pa_t_kernel(tc, q, rep, Wq, Wk, Wv, W1, b1, out):
         def evacuate(j):
             r, i = divmod(j, 2)
             if i == 0:
-                grp[r] = grp_pool.tile([P, 2048], BF16, name="grp", align_bytes=64)
+                grp[r] = grp_pool.tile([P, 2 * 2 * P * PACK], BF16, name="grp", align_bytes=64)
+            half = 2 * P * PACK
             nc.scalar.copy(
-                out=grp[r][:, i * 1024 : (i + 1) * 1024]
+                out=grp[r][:, i * half : (i + 1) * half]
                 .bitcast(F32)
                 .rearrange("p (a n u) -> p a n u", a=2, u=2),
                 in_=tb[j][:].rearrange("p (a u n) -> p a n u", a=2, u=2),
             )
 
         def quantise_x(r):
-            x_code[r] = code_pool.tile([P, 512], U32, name="x_code", align_bytes=64)
-            x_scale[r] = code_pool.tile([P, 512], U8, name="x_scale", align_bytes=64)
+            x_code[r] = code_pool.tile([P, 2 * 2 * P], U32, name="x_code", align_bytes=64)
+            x_scale[r] = code_pool.tile([P, 2 * 2 * P], U8, name="x_scale", align_bytes=64)
             nc.vector.quantize_mx(
                 out=x_code[r][:].bitcast(FP8X4), scales=x_scale[r][:], in_=grp[r][:]
             )
@@ -156,7 +160,7 @@ def tile_treehopnode_pa_t_kernel(tc, q, rep, Wq, Wk, Wv, W1, b1, out):
             r, i = divmod(j, 2)
             a = 0 if key == "q" else 1
             pool = {"q": qb_pool, "k": kb_pool, "v": vb_pool}[key]
-            bank = pool.tile([P, 512], F32, name="bank_" + key)
+            bank = pool.tile([P, BANK], F32, name="bank_" + key)
             banks[(key, j)] = bank
             c0 = (2 * i + a) * P
             for t in range(4):
@@ -170,24 +174,18 @@ def tile_treehopnode_pa_t_kernel(tc, q, rep, Wq, Wk, Wv, W1, b1, out):
                     stop=True,
                 )
 
-        def by_node(ap):
-            return ap
-
-        def flat(ap):
-            return ap
-
         def copy_q(j):
-            q_sb[j] = f32_pool.tile([P, 512], F32, name="q_sb")
-            nc.scalar.copy(out=flat(q_sb[j][:]), in_=by_node(banks[("q", j)][:]))
+            q_sb[j] = f32_pool.tile([P, BANK], F32, name="q_sb")
+            nc.scalar.copy(out=q_sb[j][:], in_=banks[("q", j)][:])
 
         def product(j):
-            prod[j] = f32_pool.tile([P, 512], F32, name="prod")
+            prod[j] = f32_pool.tile([P, BANK], F32, name="prod")
             nc.vector.tensor_tensor(
-                out=flat(prod[j][:]), in0=flat(q_sb[j][:]), in1=by_node(banks[("k", j)][:]), op=ALU.mult
+                out=prod[j][:], in0=q_sb[j][:], in1=banks[("k", j)][:], op=ALU.mult
             )
 
         def sigmoid(j):
-            gate[j] = f32_pool.tile([P, 512], F32, name="gate")
+            gate[j] = f32_pool.tile([P, BANK], F32, name="gate")
             nc.scalar.activation(
                 out=gate[j][:], in_=prod[j][:], func=ACT.Sigmoid, scale=1.0 / math.sqrt(G)
             )
@@ -195,23 +193,23 @@ def tile_treehopnode_pa_t_kernel(tc, q, rep, Wq, Wk, Wv, W1, b1, out):
         def gated(j):
             r, i = divmod(j, 2)
             if i == 0:
-                z_grp[r] = z_pool.tile([P, 1024], BF16, name="z_grp", align_bytes=64)
+                z_grp[r] = z_pool.tile([P, 2 * P * PACK], BF16, name="z_grp", align_bytes=64)
             nc.vector.tensor_tensor(
-                out=z_grp[r][:, i * 512 : (i + 1) * 512].rearrange("p (c i t) -> p c t i", i=4, t=4),
+                out=z_grp[r][:, i * BANK : (i + 1) * BANK].rearrange("p (c i t) -> p c t i", i=4, t=4),
                 in0=gate[j][:].rearrange("p (t c i) -> p c t i", t=4, i=4),
                 in1=banks[("v", j)][:].rearrange("p (t c i) -> p c t i", t=4, i=4),
                 op=ALU.mult,
             )
 
         def quantise_z(r):
-            z_code[r] = z_pool.tile([P, 256], U32, name="z_code", align_bytes=64)
-            z_scale[r] = z_pool.tile([P, 256], U8, name="z_scale", align_bytes=64)
+            z_code[r] = z_pool.tile([P, 2 * P], U32, name="z_code", align_bytes=64)
+            z_scale[r] = z_pool.tile([P, 2 * P], U8, name="z_scale", align_bytes=64)
             nc.vector.quantize_mx(
                 out=z_code[r][:].bitcast(FP8X4), scales=z_scale[r][:], in_=z_grp[r][:]
             )
 
         def layer(r):
-            o_bank[r] = ob_pool.tile([P, 512], F32, name="o_bank")
+            o_bank[r] = ob_pool.tile([P, BANK], F32, name="o_bank")
             for i in range(2):
                 nc.tensor.matmul_mx(
                     out=o_bank[r][:, i * M : (i + 1) * M],
@@ -223,8 +221,8 @@ def tile_treehopnode_pa_t_kernel(tc, q, rep, Wq, Wk, Wv, W1, b1, out):
                     stop=True,
                 )
 
-        def finish(r):
-            o_sb[r] = o_pool.tile([P, 512], F32, name="o_sb")
+        def add_bias(r):
+            o_sb[r] = o_pool.tile([P, BANK], F32, name="o_sb")
             nc.vector.tensor_tensor(
                 out=o_sb[r][:].rearrange("p (i m) -> p i m", i=2),
                 in0=o_bank[r][:].rearrange("p (i m) -> p i m", i=2),
@@ -233,60 +231,65 @@ def tile_treehopnode_pa_t_kernel(tc, q, rep, Wq, Wk, Wv, W1, b1, out):
             )
 
         def relu_store(r):
-            nc.scalar.activation(out=o_sb[r][:], in_=o_sb[r][:], func=ACT.Relu)
+            if r < PAIRS - PAIRS_WITH_RELU_ON_SCALAR:
+                nc.gpsimd.tensor_scalar(
+                    out=o_sb[r][:], in0=o_sb[r][:], scalar1=0.0, scalar2=0.0, op0=ALU.max, op1=ALU.add
+                )
+            else:
+                nc.scalar.activation(out=o_sb[r][:], in_=o_sb[r][:], func=ACT.Relu)
             nc.sync.dma_start(
                 out=out_view[:, 2 * r : 2 * r + 2, :],
                 in_=o_sb[r][:].rearrange("p (j m) -> p j m", m=M),
             )
 
-        def ok(r):
+        def live(r):
             return 0 <= r < PAIRS
 
         for r in range(-3, PAIRS + 2):
-            if ok(r - 2):
+            if live(r - 2):
                 layer(r - 2)
-            if ok(r):
+            if live(r):
                 copy_q(2 * r + 1)
                 product(2 * r)
                 sigmoid(2 * r)
-            if ok(r - 1):
+            if live(r - 1):
                 gated(2 * r - 1)
-            if ok(r):
+            if live(r):
                 project("k", 2 * r + 1)
-            if ok(r + 1):
+            if live(r + 1):
                 project("q", 2 * r + 2)
-            if ok(r - 2):
-                finish(r - 2)
-            if ok(r):
+            if live(r - 2):
+                add_bias(r - 2)
+            if live(r):
                 project("v", 2 * r)
-            if ok(r + 2):
+            if live(r + 2):
                 evacuate(2 * r + 4)
                 evacuate(2 * r + 5)
-            if ok(r + 1):
+            if live(r + 1):
                 project("q", 2 * r + 3)
-            if ok(r):
+            if live(r):
                 product(2 * r + 1)
                 sigmoid(2 * r + 1)
-            if ok(r + 1):
+            if live(r + 1):
                 project("k", 2 * r + 2)
-            if ok(r):
+            if live(r):
                 gated(2 * r)
-            if ok(r + 3):
+            if live(r + 3):
                 transposes(r + 3)
-            if ok(r):
+            if live(r):
                 project("v", 2 * r + 1)
-            if ok(r + 1):
+            if live(r + 1):
                 copy_q(2 * r + 2)
-            if ok(r - 2):
+            if live(r - 2):
                 relu_store(r - 2)
-            if ok(r - 1):
+            if live(r - 1):
                 quantise_z(r - 1)
-            if ok(r + 2):
+            if live(r + 2):
                 quantise_x(r + 2)
             if r == -2:
                 nc.vector.tensor_copy(
-                    out=w1_grp[:].rearrange("p (m j) -> p m j", j=4),
-                    in_=w1_raw[:].rearrange("p (j m) -> p m j", j=4),
+                    out=w1_grp[:].rearrange("p (m j) -> p m j", j=PACK),
+                    in_=w1_raw[:].rearrange("p (j m) -> p m j", j=PACK),
                 )
             if r == -1:
                 nc.vector.quantize_mx(

import math
from contextlib import ExitStack

import concourse.mybir as mybir
from concourse.masks import make_identity

F32 = mybir.dt.float32
BF16 = mybir.dt.bfloat16
U32 = mybir.dt.uint32
U8 = mybir.dt.uint8
FP8X4 = mybir.dt.float8_e4m3fn_x4
ALU = mybir.AluOpType
ACT = mybir.ActivationFunctionType

P = 128
PACK = 4
BANK = 512
NODES, E, G, M = 4096, 512, 512, 256
TILES = NODES // P
PAIRS = TILES // 2
FLOPS = 2 * NODES * E * 3 * G + 2 * NODES * G * M

CHUNKS = [(0, 2), (2, 4)] + [(j, j + 4) for j in range(4, TILES, 4)]

PAIRS_WITH_RELU_ON_SCALAR = 2


def tile_treehopnode_pa_t_kernel(tc, q, rep, Wq, Wk, Wv, W1, b1, out):
    nc = tc.nc
    q_view = q.rearrange("(p j) e -> p j e", j=TILES)
    rep_view = rep.rearrange("(p j) e -> p j e", j=TILES)
    out_view = out.rearrange("(p j) h m -> p j (h m)", j=TILES)

    with ExitStack() as ctx:
        const = ctx.enter_context(tc.tile_pool(name="const", bufs=1))
        grp_pool = ctx.enter_context(tc.tile_pool(name="grp_pool", bufs=3))
        code_pool = ctx.enter_context(tc.tile_pool(name="code_pool", bufs=4))
        f32_pool = ctx.enter_context(tc.tile_pool(name="f32_pool", bufs=3))
        z_pool = ctx.enter_context(tc.tile_pool(name="z_pool", bufs=3))
        o_pool = ctx.enter_context(tc.tile_pool(name="o_pool", bufs=4))
        tb_pool = ctx.enter_context(tc.psum_pool(name="tb_pool", bufs=2))
        qb_pool = ctx.enter_context(tc.psum_pool(name="qb_pool", bufs=2))
        kb_pool = ctx.enter_context(tc.psum_pool(name="kb_pool", bufs=2))
        vb_pool = ctx.enter_context(tc.psum_pool(name="vb_pool", bufs=1))
        ob_pool = ctx.enter_context(tc.psum_pool(name="ob_pool", bufs=1))
        ctx.enter_context(tc.manual_schedule())

        bias = const.tile([P, M], BF16, name="bias")
        w_raw = {}
        for key, w in (("q", Wq), ("k", Wk), ("v", Wv)):
            w_raw[key] = const.tile([P, PACK * G], BF16, name="w_raw_" + key)
            nc.sync.dma_start(
                out=w_raw[key][:].rearrange("p (u x) -> p u x", u=2),
                in_=w.rearrange("(u p e) g -> p u (e g)", u=2, e=2),
            )
        w1_raw = const.tile([P, PACK * M], BF16, name="w1_raw")
        x_raw = {}
        where = {}
        for c, (j0, j1) in enumerate(CHUNKS):
            for a, view in enumerate((q_view, rep_view)):
                x_raw[(a, c)] = const.tile([P, (j1 - j0) * E], BF16, name="x_raw_%d_%d" % (a, c))
                nc.sync.dma_start(
                    out=x_raw[(a, c)][:].rearrange("p (j e) -> p j e", e=E),
                    in_=view[:, j0:j1, :],
                )
            for j in range(j0, j1):
                where[j] = (c, j - j0)
            if c == 0:
                nc.sync.dma_start(out=w1_raw[:], in_=W1.rearrange("h (p j) m -> (h p) (j m)", j=PACK))
            if c == 2:
                nc.sync.dma_start(
                    out=bias[:], in_=b1.rearrange("h m -> (h m)").partition_broadcast(P)
                )

        ident = const.tile([P, P], F32, name="ident")
        make_identity(nc, ident[:])
        warm_in = const.tile([P, 1], F32, name="warm_in")
        warm_out = const.tile([P, 1], F32, name="warm_out")
        nc.vector.memset(warm_in[:], 0.0)
        nc.scalar.activation(out=warm_out[:], in_=warm_in[:], func=ACT.Sigmoid)

        w_grp = {}
        w_code = {}
        w_scale = {}
        for key in ("q", "k", "v"):
            w_grp[key] = const.tile([P, PACK * G], BF16, name="w_grp_" + key, align_bytes=64)
            w_code[key] = const.tile([P, G], U32, name="w_code_" + key, align_bytes=64)
            w_scale[key] = const.tile([P, G], U8, name="w_scale_" + key, align_bytes=64)
        w1_grp = const.tile([P, PACK * M], BF16, name="w1_grp", align_bytes=64)
        w1_code = const.tile([P, M], U32, name="w1_code", align_bytes=64)
        w1_scale = const.tile([P, M], U8, name="w1_scale", align_bytes=64)

        def regroup_w(key):
            src = w_raw[key][:].rearrange("p (j c t) -> p t c j", j=PACK, t=4)
            dst = w_grp[key][:].rearrange("p (t c j) -> p t c j", t=4, j=PACK)
            nc.vector.tensor_copy(out=dst[:, 0:2], in_=src[:, 0:2])
            nc.scalar.copy(out=dst[:, 2:4], in_=src[:, 2:4])

        def quantise_w(key):
            nc.vector.quantize_mx(
                out=w_code[key][:].bitcast(FP8X4), scales=w_scale[key][:], in_=w_grp[key][:]
            )

        regroup_w("q")
        regroup_w("k")
        quantise_w("q")
        regroup_w("v")
        quantise_w("k")
        quantise_w("v")

        tb = {}
        grp = {}
        x_code = {}
        x_scale = {}
        banks = {}
        q_sb = {}
        prod = {}
        gate = {}
        z_grp = {}
        z_code = {}
        z_scale = {}
        o_bank = {}
        o_sb = {}

        def transposes(r):
            for j in (2 * r, 2 * r + 1):
                c, place = where[j]
                tb[j] = tb_pool.tile([P, BANK], F32, name="tb")
                for a in range(2):
                    words = x_raw[(a, c)][:].bitcast(F32)
                    for u in range(2):
                        s = 2 * a + u
                        w0 = place * (E // 2) + u * P
                        nc.tensor.transpose(
                            out=tb[j][:, s * P : (s + 1) * P],
                            in_=words[:, w0 : w0 + P],
                            identity=ident[:],
                        )

        def evacuate(j):
            r, i = divmod(j, 2)
            if i == 0:
                grp[r] = grp_pool.tile([P, 2 * 2 * P * PACK], BF16, name="grp", align_bytes=64)
            half = 2 * P * PACK
            nc.scalar.copy(
                out=grp[r][:, i * half : (i + 1) * half]
                .bitcast(F32)
                .rearrange("p (a n u) -> p a n u", a=2, u=2),
                in_=tb[j][:].rearrange("p (a u n) -> p a n u", a=2, u=2),
            )

        def quantise_x(r):
            x_code[r] = code_pool.tile([P, 2 * 2 * P], U32, name="x_code", align_bytes=64)
            x_scale[r] = code_pool.tile([P, 2 * 2 * P], U8, name="x_scale", align_bytes=64)
            nc.vector.quantize_mx(
                out=x_code[r][:].bitcast(FP8X4), scales=x_scale[r][:], in_=grp[r][:]
            )

        def project(key, j):
            r, i = divmod(j, 2)
            a = 0 if key == "q" else 1
            pool = {"q": qb_pool, "k": kb_pool, "v": vb_pool}[key]
            bank = pool.tile([P, BANK], F32, name="bank_" + key)
            banks[(key, j)] = bank
            c0 = (2 * i + a) * P
            for t in range(4):
                nc.tensor.matmul_mx(
                    out=bank[:, t * P : (t + 1) * P],
                    lhsT=w_code[key][:, t * P : (t + 1) * P].bitcast(FP8X4),
                    lhsT_scale=w_scale[key][:, t * P : (t + 1) * P],
                    rhs=x_code[r][:, c0 : c0 + P].bitcast(FP8X4),
                    rhs_scale=x_scale[r][:, c0 : c0 + P],
                    start=True,
                    stop=True,
                )

        def copy_q(j):
            q_sb[j] = f32_pool.tile([P, BANK], F32, name="q_sb")
            nc.scalar.copy(out=q_sb[j][:], in_=banks[("q", j)][:])

        def product(j):
            prod[j] = f32_pool.tile([P, BANK], F32, name="prod")
            nc.vector.tensor_tensor(
                out=prod[j][:], in0=q_sb[j][:], in1=banks[("k", j)][:], op=ALU.mult
            )

        def sigmoid(j):
            gate[j] = f32_pool.tile([P, BANK], F32, name="gate")
            nc.scalar.activation(
                out=gate[j][:], in_=prod[j][:], func=ACT.Sigmoid, scale=1.0 / math.sqrt(G)
            )

        def gated(j):
            r, i = divmod(j, 2)
            if i == 0:
                z_grp[r] = z_pool.tile([P, 2 * P * PACK], BF16, name="z_grp", align_bytes=64)
            nc.vector.tensor_tensor(
                out=z_grp[r][:, i * BANK : (i + 1) * BANK].rearrange("p (c i t) -> p c t i", i=4, t=4),
                in0=gate[j][:].rearrange("p (t c i) -> p c t i", t=4, i=4),
                in1=banks[("v", j)][:].rearrange("p (t c i) -> p c t i", t=4, i=4),
                op=ALU.mult,
            )

        def quantise_z(r):
            z_code[r] = z_pool.tile([P, 2 * P], U32, name="z_code", align_bytes=64)
            z_scale[r] = z_pool.tile([P, 2 * P], U8, name="z_scale", align_bytes=64)
            nc.vector.quantize_mx(
                out=z_code[r][:].bitcast(FP8X4), scales=z_scale[r][:], in_=z_grp[r][:]
            )

        def layer(r):
            o_bank[r] = ob_pool.tile([P, BANK], F32, name="o_bank")
            for i in range(2):
                nc.tensor.matmul_mx(
                    out=o_bank[r][:, i * M : (i + 1) * M],
                    lhsT=z_code[r][:, i * P : (i + 1) * P].bitcast(FP8X4),
                    lhsT_scale=z_scale[r][:, i * P : (i + 1) * P],
                    rhs=w1_code[:].bitcast(FP8X4),
                    rhs_scale=w1_scale[:],
                    start=True,
                    stop=True,
                )

        def add_bias(r):
            o_sb[r] = o_pool.tile([P, BANK], F32, name="o_sb")
            nc.vector.tensor_tensor(
                out=o_sb[r][:].rearrange("p (i m) -> p i m", i=2),
                in0=o_bank[r][:].rearrange("p (i m) -> p i m", i=2),
                in1=bias[:].unsqueeze(1).to_broadcast([P, 2, M]),
                op=ALU.add,
            )

        def relu_store(r):
            if r < PAIRS - PAIRS_WITH_RELU_ON_SCALAR:
                nc.gpsimd.tensor_scalar(
                    out=o_sb[r][:], in0=o_sb[r][:], scalar1=0.0, scalar2=0.0, op0=ALU.max, op1=ALU.add
                )
            else:
                nc.scalar.activation(out=o_sb[r][:], in_=o_sb[r][:], func=ACT.Relu)
            nc.sync.dma_start(
                out=out_view[:, 2 * r : 2 * r + 2, :],
                in_=o_sb[r][:].rearrange("p (j m) -> p j m", m=M),
            )

        def live(r):
            return 0 <= r < PAIRS

        for r in range(-3, PAIRS + 2):
            if live(r - 2):
                layer(r - 2)
            if live(r):
                copy_q(2 * r + 1)
                product(2 * r)
                sigmoid(2 * r)
            if live(r - 1):
                gated(2 * r - 1)
            if live(r):
                project("k", 2 * r + 1)
            if live(r + 1):
                project("q", 2 * r + 2)
            if live(r - 2):
                add_bias(r - 2)
            if live(r):
                project("v", 2 * r)
            if live(r + 2):
                evacuate(2 * r + 4)
                evacuate(2 * r + 5)
            if live(r + 1):
                project("q", 2 * r + 3)
            if live(r):
                product(2 * r + 1)
                sigmoid(2 * r + 1)
            if live(r + 1):
                project("k", 2 * r + 2)
            if live(r):
                gated(2 * r)
            if live(r + 3):
                transposes(r + 3)
            if live(r):
                project("v", 2 * r + 1)
            if live(r + 1):
                copy_q(2 * r + 2)
            if live(r - 2):
                relu_store(r - 2)
            if live(r - 1):
                quantise_z(r - 1)
            if live(r + 2):
                quantise_x(r + 2)
            if r == -2:
                nc.vector.tensor_copy(
                    out=w1_grp[:].rearrange("p (m j) -> p m j", j=PACK),
                    in_=w1_raw[:].rearrange("p (j m) -> p m j", j=PACK),
                )
            if r == -1:
                nc.vector.quantize_mx(
                    out=w1_code[:].bitcast(FP8X4), scales=w1_scale[:], in_=w1_grp[:]
                )
